import numpy as np
import ml_dtypes


def mxq(x, axis, fmt="e4m3"):
    dtype, down = {"e4m3": (ml_dtypes.float8_e4m3fn, 7), "e5m2": (ml_dtypes.float8_e5m2, 14)}[fmt]
    v = np.moveaxis(np.asarray(x, np.float32).astype(ml_dtypes.bfloat16).astype(np.float64), axis, -1)
    blocks = v.reshape(v.shape[:-1] + (-1, 32))
    amax = np.abs(blocks).max(-1, keepdims=True)
    byte = np.maximum(np.where(amax > 0, np.frexp(amax)[1] - 1 + 127, 0) - down, 1)
    scale = np.exp2(byte - 127.0)
    codes = (blocks / scale).astype(np.float32).astype(dtype).astype(np.float64)
    return np.moveaxis((codes * scale).reshape(v.shape), -1, axis)


WIDE = False


def mx_kscale(k):
    if not WIDE:
        return np.ones(k)
    levels = np.array([10, -10, 5, -5, 0])
    a = np.random.permutation(np.resize(levels, k // 512 * 4)).reshape(k // 512, 4)
    idx = np.arange(k)
    return np.exp2(a[idx // 512, idx % 128 // 32])


BF16 = ml_dtypes.bfloat16


def bf(x):
    return np.asarray(x, np.float32).astype(BF16)


def f64(x):
    return np.asarray(x).astype(np.float64)


B, S, I, Q = 512, 8, 1024, 1024
LN_EPS = 1e-5


def setup_inputs():
    s = mx_kscale(I)
    return {"language_features": bf(np.random.standard_normal((B, I)) * s),
            "W": bf(np.random.standard_normal((S, I, Q)) / np.sqrt(I) / s[None, :, None]),
            "b": bf(np.random.standard_normal((S, Q)) * 0.2),
            "amplitude_weights": bf(np.random.standard_normal((S, Q))),
            "phase_weights": bf(np.random.standard_normal((S, Q))),
            "ln_gamma": bf(1.0 + 0.1 * np.random.standard_normal(Q)),
            "ln_beta": bf(0.1 * np.random.standard_normal(Q))}


def reference(language_features, W, b, amplitude_weights, phase_weights, ln_gamma, ln_beta):
    xq = mxq(f64(language_features), 1, "e4m3")
    wq = mxq(f64(W), 1, "e4m3")
    states = (xq @ wq).transpose(1, 0, 2) + f64(b)[None, :, :]
    a = f64(amplitude_weights)
    e = np.exp(a - a.max(axis=0, keepdims=True))
    amplitudes = e / e.sum(axis=0, keepdims=True)
    mix = amplitudes * np.cos(f64(phase_weights))
    sup = states * mix[None, :, :]
    mean = sup.mean(axis=-1, keepdims=True)
    var = sup.var(axis=-1, keepdims=True)
    return (sup - mean) * (1.0 / np.sqrt(var + LN_EPS)) * f64(ln_gamma) + f64(ln_beta)

@@ -1,0 +1,334 @@
+import math
+from contextlib import ExitStack
+
+import concourse.mybir as mybir
+from concourse.masks import make_identity
+
+FP8X4 = mybir.dt.float8_e4m3fn_x4
+BF16 = mybir.dt.bfloat16
+F32 = mybir.dt.float32
+I32 = mybir.dt.int32
+U32 = mybir.dt.uint32
+U8 = mybir.dt.uint8
+ACT = mybir.ActivationFunctionType
+ALU = mybir.AluOpType
+AX = mybir.AxisListType
+
+P = 128
+B, S, I, Q = 512, 8, 1024, 1024
+LN_EPS = 1e-5
+FLOPS = 2 * B * S * I * Q
+
+PASSES = I // 512
+QT = Q // P
+BT = B // P
+GROUPS = S * BT
+V_COLS = 320
+LEAD_MX = 5
+LEAD_RG = 11
+
+TWO_PI_HI = 6.28125
+TWO_PI_LO = 2.0 * math.pi - 6.28125
+PI_BELOW = 3.1415925
+
+
+def tile_quantumsuperposition_kernel(
+    tc, language_features, W, b, amplitude_weights, phase_weights, ln_gamma, ln_beta, out
+):
+    nc = tc.nc
+    with ExitStack() as ctx:
+        const = ctx.enter_context(tc.tile_pool(name="const", bufs=1))
+        small = ctx.enter_context(tc.tile_pool(name="small", bufs=1))
+        raw_pool = ctx.enter_context(tc.tile_pool(name="raw", bufs=8))
+        wg_pool = ctx.enter_context(tc.tile_pool(name="wg", bufs=3))
+        code_pool = ctx.enter_context(tc.tile_pool(name="codes", bufs=4))
+        supt_pool = ctx.enter_context(tc.tile_pool(name="supt", bufs=2))
+        y_pool = ctx.enter_context(tc.tile_pool(name="y", bufs=6))
+        stat_pool = ctx.enter_context(tc.tile_pool(name="stat", bufs=4))
+        ps_acc = ctx.enter_context(tc.psum_pool(name="ps_acc", bufs=3))
+        ps_sup = ctx.enter_context(tc.psum_pool(name="ps_sup", bufs=4))
+        ps_sum = ctx.enter_context(tc.psum_pool(name="ps_sum", bufs=1))
+
+        x_sb = []
+        for bt in range(BT):
+            xt_sb = const.tile([P, I], BF16, name="x_sb%d" % bt)
+            nc.sync.dma_start(out=xt_sb[:], in_=language_features[bt * P : (bt + 1) * P, :])
+            x_sb.append(xt_sb)
+
+        par_a = small.tile([P, P], BF16, name="par_a")
+        par_b = small.tile([P, P], BF16, name="par_b")
+        nc.vector.memset(par_b[64:128, :], 0.0)
+        nc.scalar.dma_start(out=par_a[0:64, :], in_=amplitude_weights.rearrange("s (t q) -> (s t) q", q=P))
+        nc.scalar.dma_start(out=par_a[64:128, :], in_=phase_weights.rearrange("s (t q) -> (s t) q", q=P))
+        nc.scalar.dma_start(out=par_b[0:64, :], in_=b.rearrange("s (t q) -> (s t) q", q=P))
+
+        raw = {}
+
+        def load_unit(u):
+            s, c = divmod(u, PASSES)
+            t = raw_pool.tile([P, 4, Q], BF16, name="raw%d" % u, tag="raw")
+            nc.sync.dma_start(
+                out=t[:], in_=W[s, c * 512 : (c + 1) * 512, :].rearrange("(p j) q -> p j q", j=4)
+            )
+            raw[u] = t
+
+        for u in range(4):
+            load_unit(u)
+        gamma_bc = const.tile([P, Q], BF16, name="gamma_bc")
+        beta_bc = const.tile([P, Q], BF16, name="beta_bc")
+        nc.sync.dma_start(out=gamma_bc[:], in_=ln_gamma.partition_broadcast(P))
+        nc.sync.dma_start(out=beta_bc[:], in_=ln_beta.partition_broadcast(P))
+        for u in range(4, 8):
+            load_unit(u)
+
+        ident = const.tile([P, P], F32, name="ident")
+        make_identity(nc, ident[:])
+        neghalf = const.tile([P, 1], F32, name="neghalf")
+        nc.vector.memset(neghalf[:], -0.5)
+
+        xc = const.tile([P, PASSES, B], U32, name="xc", align_bytes=64)
+        xs = const.tile([P, PASSES, B], U8, name="xs", align_bytes=64)
+        xw = [t[:].bitcast(F32).rearrange("p (g w u) -> p g u w", g=PASSES, u=2) for t in x_sb]
+        for g in range(PASSES):
+            xg = const.tile([P, 4 * B], BF16, name="xg%d" % g, align_bytes=64)
+            xg_words = xg[:].bitcast(F32).rearrange("p (r u) -> p r u", u=2)
+            for h in range(2):
+                xt = ps_sup.tile([P, 2, 256], F32, name="xt%d%d" % (g, h), tag="sup")
+                for bl in range(2):
+                    for u in range(2):
+                        nc.tensor.transpose(
+                            out=xt[:, u, bl * P : (bl + 1) * P], in_=xw[2 * h + bl][:, g, u, :], identity=ident[:]
+                        )
+                dst = xg_words[:, h * 256 : (h + 1) * 256, :]
+                src = xt[:].rearrange("p u r -> p r u")
+                if h == 0:
+                    nc.vector.tensor_copy(out=dst, in_=src)
+                else:
+                    nc.scalar.copy(out=dst, in_=src)
+            nc.vector.quantize_mx(out=xc[:, g, :].bitcast(FP8X4), scales=xs[:, g, :], in_=xg[:])
+
+        par_af = small.tile([P, P], F32, name="par_af")
+        par_bf = small.tile([P, P], F32, name="par_bf")
+        nc.vector.tensor_copy(out=par_af[:], in_=par_a[:])
+        nc.vector.tensor_copy(out=par_bf[:], in_=par_b[:])
+        par_ps = ps_acc.tile([P, 512], F32, name="par_ps", tag="acc")
+        nc.tensor.transpose(out=par_ps[:, 0:P], in_=par_af[:], identity=ident[:])
+        nc.tensor.transpose(out=par_ps[:, P : 2 * P], in_=par_bf[:], identity=ident[:])
+        prm = small.tile([P, 192], F32, name="prm")
+        nc.vector.tensor_copy(out=prm[:], in_=par_ps[:, 0:192])
+        amp_t = prm[:, 0:64]
+        pha_t = prm[:, 64:128]
+        bias_t = prm[:, 128:192]
+
+        def st(ap):
+            return ap.rearrange("p (s t) -> p s t", s=S)
+
+        def ts(ap):
+            return ap.rearrange("p (s t) -> p t s", s=S)
+
+        def over_s(ap):
+            return ap.unsqueeze(1).to_broadcast([P, S, QT])
+
+        amax = small.tile([P, QT], F32, name="amax")
+        nc.vector.tensor_reduce(out=amax[:], in_=ts(amp_t), axis=AX.X, op=ALU.max)
+        ash = small.tile([P, 64], F32, name="ash")
+        nc.vector.tensor_tensor(out=st(ash[:]), in0=st(amp_t), in1=over_s(amax[:]), op=ALU.subtract)
+        aex = small.tile([P, 64], F32, name="aex")
+        nc.scalar.activation(out=aex[:], in_=ash[:], func=ACT.Exp)
+        asum = small.tile([P, QT], F32, name="asum")
+        nc.vector.tensor_reduce(out=asum[:], in_=ts(aex[:]), axis=AX.X, op=ALU.add)
+        arec = small.tile([P, QT], F32, name="arec")
+        nc.vector.reciprocal(out=arec[:], in_=asum[:])
+
+        turns = small.tile([P, 64], F32, name="turns")
+        nc.vector.tensor_scalar(
+            out=turns[:], in0=pha_t, scalar1=1.0 / (2.0 * math.pi), scalar2=0.25, op0=ALU.mult, op1=ALU.add
+        )
+        turns_i = small.tile([P, 64], I32, name="turns_i")
+        nc.vector.tensor_copy(out=turns_i[:], in_=turns[:])
+        turns_f = small.tile([P, 64], F32, name="turns_f")
+        nc.vector.tensor_copy(out=turns_f[:], in_=turns_i[:])
+        ang0 = small.tile([P, 64], F32, name="ang0")
+        nc.vector.tensor_scalar(out=ang0[:], in0=pha_t, scalar1=0.5 * math.pi, scalar2=None, op0=ALU.add)
+        ang1 = small.tile([P, 64], F32, name="ang1")
+        nc.vector.scalar_tensor_tensor(
+            out=ang1[:], in0=turns_f[:], scalar=-TWO_PI_HI, in1=ang0[:], op0=ALU.mult, op1=ALU.add
+        )
+        ang2 = small.tile([P, 64], F32, name="ang2")
+        nc.vector.scalar_tensor_tensor(
+            out=ang2[:], in0=turns_f[:], scalar=-TWO_PI_LO, in1=ang1[:], op0=ALU.mult, op1=ALU.add
+        )
+        fix1 = small.tile([P, 64], F32, name="fix1")
+        nc.vector.tensor_scalar(
+            out=fix1[:], in0=ang2[:], scalar1=math.pi, scalar2=-2.0 * math.pi, op0=ALU.is_gt, op1=ALU.mult
+        )
+        ang3 = small.tile([P, 64], F32, name="ang3")
+        nc.vector.tensor_tensor(out=ang3[:], in0=ang2[:], in1=fix1[:], op=ALU.add)
+        fix2 = small.tile([P, 64], F32, name="fix2")
+        nc.vector.tensor_scalar(
+            out=fix2[:], in0=ang3[:], scalar1=-math.pi, scalar2=2.0 * math.pi, op0=ALU.is_lt, op1=ALU.mult
+        )
+        ang4 = small.tile([P, 64], F32, name="ang4")
+        nc.vector.tensor_tensor(out=ang4[:], in0=ang3[:], in1=fix2[:], op=ALU.add)
+        ang5 = small.tile([P, 64], F32, name="ang5")
+        nc.vector.tensor_scalar(
+            out=ang5[:], in0=ang4[:], scalar1=-PI_BELOW, scalar2=PI_BELOW, op0=ALU.max, op1=ALU.min
+        )
+        cosv = small.tile([P, 64], F32, name="cosv")
+        nc.scalar.activation(out=cosv[:], in_=ang5[:], func=ACT.Sin)
+
+        ampl = small.tile([P, 64], F32, name="ampl")
+        nc.vector.tensor_tensor(out=st(ampl[:]), in0=st(aex[:]), in1=over_s(arec[:]), op=ALU.mult)
+        mix_t = const.tile([P, 64], F32, name="mix_t")
+        nc.vector.tensor_tensor(out=mix_t[:], in0=ampl[:], in1=cosv[:], op=ALU.mult)
+        bmix_t = const.tile([P, 64], F32, name="bmix_t")
+        nc.vector.tensor_tensor(out=bmix_t[:], in0=bias_t, in1=mix_t[:], op=ALU.mult)
+
+        wg = {}
+        wc = {}
+        ws = {}
+        supt = {}
+        sup = {}
+        ysb = {}
+        negmean = {}
+        varsum = {}
+        rstd = {}
+
+        def regroup(u, h):
+            if h == 0:
+                wg[u] = wg_pool.tile([P, Q, 4], BF16, name="wg%d" % u, tag="wg", align_bytes=64)
+            lo = h * 512
+            mid = lo + V_COLS
+            hi = lo + 512
+            nc.vector.tensor_copy(
+                out=wg[u][:, lo:mid, :].rearrange("p (c i) t -> p c t i", i=4),
+                in_=raw[u][:, :, lo:mid].rearrange("p t (c i) -> p c t i", i=4),
+            )
+            nc.scalar.copy(
+                out=wg[u][:, mid:hi, :].rearrange("p (c i) t -> p c t i", i=4),
+                in_=raw[u][:, :, mid:hi].rearrange("p t (c i) -> p c t i", i=4),
+            )
+
+        def quantise(u):
+            s, c = divmod(u, PASSES)
+            if c == 0:
+                wc[s] = code_pool.tile([P, PASSES, Q], U32, name="wc%d" % s, tag="wc", align_bytes=64)
+                ws[s] = code_pool.tile([P, PASSES, Q], U8, name="ws%d" % s, tag="ws", align_bytes=64)
+            nc.vector.quantize_mx(
+                out=wc[s][:, c, :].bitcast(FP8X4),
+                scales=ws[s][:, c, :],
+                in_=wg[u][:].rearrange("p w j -> p (w j)"),
+            )
+
+        def states(s, qt):
+            if qt == 0:
+                supt[s] = supt_pool.tile([P, QT, B], F32, name="supt%d" % s, tag="supt")
+            cols = slice(qt * P, (qt + 1) * P)
+            acc = ps_acc.tile([P, B], F32, name="acc%d_%d" % (s, qt), tag="acc")
+            for c in range(PASSES):
+                nc.tensor.matmul_mx(
+                    out=acc[:],
+                    lhsT=wc[s][:, c, cols].bitcast(FP8X4),
+                    lhsT_scale=ws[s][:, c, cols],
+                    rhs=xc[:, c, :].bitcast(FP8X4),
+                    rhs_scale=xs[:, c, :],
+                    start=(c == 0),
+                    stop=(c == PASSES - 1),
+                )
+            col = s * QT + qt
+            nc.scalar.activation(
+                out=supt[s][:, qt, :],
+                in_=acc[:],
+                func=ACT.Identity,
+                scale=mix_t[:, col : col + 1],
+                bias=bmix_t[:, col : col + 1],
+            )
+
+        sums = {}
+
+        def turn(n):
+            s, bt = divmod(n, BT)
+            rows = slice(bt * P, (bt + 1) * P)
+            sup[n] = [ps_sup.tile([P, 512], F32, name="sup%d_%d" % (n, h), tag="sup") for h in range(2)]
+            sums[n] = ps_sum.tile([P, P], F32, name="sums%d" % n, tag="sums")
+            for qt in range(QT):
+                nc.tensor.transpose(
+                    out=sup[n][qt // 4][:, (qt % 4) * P : (qt % 4 + 1) * P], in_=supt[s][:, qt, rows], identity=ident[:]
+                )
+            for qt in range(QT):
+                nc.tensor.matmul(
+                    out=sums[n][:],
+                    lhsT=supt[s][:, qt, rows],
+                    rhs=ident[:],
+                    start=(qt == 0),
+                    stop=(qt == QT - 1),
+                    is_transpose=True,
+                )
+
+        def moments(n):
+            junk = stat_pool.tile([P, P], F32, name="junk%d" % n, tag="junk")
+            negmean[n] = stat_pool.tile([P, 1], F32, name="negmean%d" % n, tag="negmean")
+            varsum[n] = stat_pool.tile([P, 2], F32, name="varsum%d" % n, tag="varsum")
+            ysb[n] = y_pool.tile([P, Q], F32, name="y%d" % n, tag="y")
+            nc.scalar.activation(
+                out=junk[:], in_=sums[n][:], func=ACT.Copy, scale=-1.0 / Q, accum_out=negmean[n][:]
+            )
+            for h in range(2):
+                nc.scalar.activation(
+                    out=ysb[n][:, h * 512 : (h + 1) * 512],
+                    in_=sup[n][h][:],
+                    func=ACT.Square,
+                    bias=negmean[n][:],
+                    accum_out=varsum[n][:, h : h + 1],
+                )
+
+        def centre(n):
+            for h in range(2):
+                half = slice(h * 512, (h + 1) * 512)
+                nc.vector.scalar_tensor_tensor(
+                    out=ysb[n][:, half],
+                    in0=sup[n][h][:],
+                    scalar=negmean[n][:],
+                    in1=gamma_bc[:, half],
+                    op0=ALU.add,
+                    op1=ALU.mult,
+                )
+
+        def inverse_std(n):
+            tot = stat_pool.tile([P, 1], F32, name="tot%d" % n, tag="tot")
+            vare = stat_pool.tile([P, 1], F32, name="vare%d" % n, tag="vare")
+            rstd[n] = stat_pool.tile([P, 1], F32, name="rstd%d" % n, tag="rstd")
+            nc.gpsimd.tensor_tensor(out=tot[:], in0=varsum[n][:, 0:1], in1=varsum[n][:, 1:2], op=ALU.add)
+            nc.gpsimd.tensor_scalar(
+                out=vare[:], in0=tot[:], scalar1=1.0 / Q, scalar2=LN_EPS, op0=ALU.mult, op1=ALU.add
+            )
+            nc.gpsimd.tensor_tensor(out=rstd[n][:], in0=vare[:], in1=neghalf[:], op=ALU.pow)
+
+        def finish(n):
+            s, bt = divmod(n, BT)
+            nc.vector.scalar_tensor_tensor(
+                out=ysb[n][:], in0=ysb[n][:], scalar=rstd[n][:], in1=beta_bc[:], op0=ALU.mult, op1=ALU.add
+            )
+            nc.sync.dma_start(out=out[bt * P : (bt + 1) * P, s, :], in_=ysb[n][:])
+
+        for n in range(-LEAD_RG, GROUPS + 1):
+            if 0 <= n + 1 < GROUPS:
+                turn(n + 1)
+            if 0 <= n < GROUPS:
+                moments(n)
+            if 0 <= n - 1:
+                finish(n - 1)
+            m = n + LEAD_MX
+            if 0 <= m < GROUPS:
+                states(m // 4, 2 * (m % 4))
+                states(m // 4, 2 * (m % 4) + 1)
+            r = n + LEAD_RG
+            if r < 2 * S * PASSES:
+                regroup(r // 2, r % 2)
+                if r % 2 == 1 and r // 2 + 8 < S * PASSES:
+                    load_unit(r // 2 + 8)
+            if r >= 2 and r % 2 == 0 and r <= 2 * S * PASSES:
+                quantise(r // 2 - 1)
+            if 0 <= n < GROUPS:
+                centre(n)
+                inverse_std(n)

@@ -23,9 +23,9 @@ PASSES = I // 512
 QT = Q // P
 BT = B // P
 GROUPS = S * BT
-V_COLS = 320
 LEAD_MX = 5
 LEAD_RG = 11
+EARLY = 12
 
 TWO_PI_HI = 6.28125
 TWO_PI_LO = 2.0 * math.pi - 6.28125
@@ -45,22 +45,10 @@ def tile_quantumsuperposition_kernel(
         supt_pool = ctx.enter_context(tc.tile_pool(name="supt", bufs=2))
         y_pool = ctx.enter_context(tc.tile_pool(name="y", bufs=6))
         stat_pool = ctx.enter_context(tc.tile_pool(name="stat", bufs=4))
-        ps_acc = ctx.enter_context(tc.psum_pool(name="ps_acc", bufs=3))
+        ps_acc = ctx.enter_context(tc.psum_pool(name="ps_acc", bufs=2))
         ps_sup = ctx.enter_context(tc.psum_pool(name="ps_sup", bufs=4))
         ps_sum = ctx.enter_context(tc.psum_pool(name="ps_sum", bufs=1))
-
-        x_sb = []
-        for bt in range(BT):
-            xt_sb = const.tile([P, I], BF16, name="x_sb%d" % bt)
-            nc.sync.dma_start(out=xt_sb[:], in_=language_features[bt * P : (bt + 1) * P, :])
-            x_sb.append(xt_sb)
-
-        par_a = small.tile([P, P], BF16, name="par_a")
-        par_b = small.tile([P, P], BF16, name="par_b")
-        nc.vector.memset(par_b[64:128, :], 0.0)
-        nc.scalar.dma_start(out=par_a[0:64, :], in_=amplitude_weights.rearrange("s (t q) -> (s t) q", q=P))
-        nc.scalar.dma_start(out=par_a[64:128, :], in_=phase_weights.rearrange("s (t q) -> (s t) q", q=P))
-        nc.scalar.dma_start(out=par_b[0:64, :], in_=b.rearrange("s (t q) -> (s t) q", q=P))
+        ps_beta = ctx.enter_context(tc.psum_pool(name="ps_beta", bufs=1))
 
         raw = {}
 
@@ -72,12 +60,29 @@ def tile_quantumsuperposition_kernel(
             )
             raw[u] = t
 
-        for u in range(4):
+        load_unit(0)
+        x_sb = []
+        for bt in range(BT):
+            xt_sb = const.tile([P, I], BF16, name="x_sb%d" % bt)
+            nc.sync.dma_start(out=xt_sb[:], in_=language_features[bt * P : (bt + 1) * P, :])
+            x_sb.append(xt_sb)
+
+        par_a = small.tile([P, P], BF16, name="par_a")
+        par_b = small.tile([P, P], BF16, name="par_b")
+        beta_row = small.tile([P, Q], BF16, name="beta_row")
+        ones_bf = small.tile([P, P], BF16, name="ones_bf")
+        nc.vector.memset(par_b[64:128, :], 0.0)
+        nc.vector.memset(beta_row[:], 0.0)
+        nc.vector.memset(ones_bf[:], 1.0)
+        nc.scalar.dma_start(out=par_a[0:64, :], in_=amplitude_weights.rearrange("s (t q) -> (s t) q", q=P))
+        nc.scalar.dma_start(out=par_a[64:128, :], in_=phase_weights.rearrange("s (t q) -> (s t) q", q=P))
+        nc.scalar.dma_start(out=par_b[0:64, :], in_=b.rearrange("s (t q) -> (s t) q", q=P))
+        nc.scalar.dma_start(out=beta_row[0:1, :], in_=ln_beta.rearrange("(o q) -> o q", o=1))
+
+        for u in range(1, 4):
             load_unit(u)
-        gamma_bc = const.tile([P, Q], BF16, name="gamma_bc")
-        beta_bc = const.tile([P, Q], BF16, name="beta_bc")
-        nc.sync.dma_start(out=gamma_bc[:], in_=ln_gamma.partition_broadcast(P))
-        nc.sync.dma_start(out=beta_bc[:], in_=ln_beta.partition_broadcast(P))
+        gamma_raw = small.tile([P, Q], BF16, name="gamma_raw")
+        nc.sync.dma_start(out=gamma_raw[:], in_=ln_gamma.partition_broadcast(P))
         for u in range(4, 8):
             load_unit(u)
 
@@ -85,6 +90,14 @@ def tile_quantumsuperposition_kernel(
         make_identity(nc, ident[:])
         neghalf = const.tile([P, 1], F32, name="neghalf")
         nc.vector.memset(neghalf[:], -0.5)
+        gamma_bc = const.tile([P, Q], BF16, name="gamma_bc")
+        nc.gpsimd.tensor_scalar(
+            out=gamma_bc[:], in0=gamma_raw[:], scalar1=math.sqrt(Q), scalar2=0.0, op0=ALU.mult, op1=ALU.add
+        )
+        beta_ps = ps_beta.tile([P, Q], BF16, name="beta_ps")
+        for h in range(2):
+            half = slice(h * 512, (h + 1) * 512)
+            nc.tensor.matmul(out=beta_ps[:, half], lhsT=ones_bf[:], rhs=beta_row[:, half], start=True, stop=True)
 
         xc = const.tile([P, PASSES, B], U32, name="xc", align_bytes=64)
         xs = const.tile([P, PASSES, B], U8, name="xs", align_bytes=64)
@@ -197,17 +210,28 @@ def tile_quantumsuperposition_kernel(
         def regroup(u, h):
             if h == 0:
                 wg[u] = wg_pool.tile([P, Q, 4], BF16, name="wg%d" % u, tag="wg", align_bytes=64)
+            g_cols, s_cols = (128, 192) if 2 * u + h < EARLY else (384, 128)
             lo = h * 512
-            mid = lo + V_COLS
+            m1 = lo + g_cols
+            m2 = m1 + s_cols
             hi = lo + 512
-            nc.vector.tensor_copy(
-                out=wg[u][:, lo:mid, :].rearrange("p (c i) t -> p c t i", i=4),
-                in_=raw[u][:, :, lo:mid].rearrange("p t (c i) -> p c t i", i=4),
+            nc.gpsimd.tensor_scalar(
+                out=wg[u][:, lo:m1, :],
+                in0=raw[u][:, :, lo:m1].rearrange("p t w -> p w t"),
+                scalar1=1.0,
+                scalar2=0.0,
+                op0=ALU.mult,
+                op1=ALU.add,
             )
             nc.scalar.copy(
-                out=wg[u][:, mid:hi, :].rearrange("p (c i) t -> p c t i", i=4),
-                in_=raw[u][:, :, mid:hi].rearrange("p t (c i) -> p c t i", i=4),
+                out=wg[u][:, m1:m2, :].rearrange("p (c i) t -> p c t i", i=4),
+                in_=raw[u][:, :, m1:m2].rearrange("p t (c i) -> p c t i", i=4),
             )
+            if m2 < hi:
+                nc.vector.tensor_copy(
+                    out=wg[u][:, m2:hi, :].rearrange("p (c i) t -> p c t i", i=4),
+                    in_=raw[u][:, :, m2:hi].rearrange("p t (c i) -> p c t i", i=4),
+                )
 
         def quantise(u):
             s, c = divmod(u, PASSES)
@@ -296,18 +320,21 @@ def tile_quantumsuperposition_kernel(
 
         def inverse_std(n):
             tot = stat_pool.tile([P, 1], F32, name="tot%d" % n, tag="tot")
-            vare = stat_pool.tile([P, 1], F32, name="vare%d" % n, tag="vare")
             rstd[n] = stat_pool.tile([P, 1], F32, name="rstd%d" % n, tag="rstd")
-            nc.gpsimd.tensor_tensor(out=tot[:], in0=varsum[n][:, 0:1], in1=varsum[n][:, 1:2], op=ALU.add)
             nc.gpsimd.tensor_scalar(
-                out=vare[:], in0=tot[:], scalar1=1.0 / Q, scalar2=LN_EPS, op0=ALU.mult, op1=ALU.add
+                out=tot[:],
+                in0=varsum[n][:, 0:1],
+                scalar1=varsum[n][:, 1:2],
+                scalar2=Q * LN_EPS,
+                op0=ALU.add,
+                op1=ALU.add,
             )
-            nc.gpsimd.tensor_tensor(out=rstd[n][:], in0=vare[:], in1=neghalf[:], op=ALU.pow)
+            nc.gpsimd.tensor_tensor(out=rstd[n][:], in0=tot[:], in1=neghalf[:], op=ALU.pow)
 
         def finish(n):
             s, bt = divmod(n, BT)
             nc.vector.scalar_tensor_tensor(
-                out=ysb[n][:], in0=ysb[n][:], scalar=rstd[n][:], in1=beta_bc[:], op0=ALU.mult, op1=ALU.add
+                out=ysb[n][:], in0=ysb[n][:], scalar=rstd[n][:], in1=beta_ps[:], op0=ALU.mult, op1=ALU.add
             )
             nc.sync.dma_start(out=out[bt * P : (bt + 1) * P, s, :], in_=ysb[n][:])
 

@@ -23,9 +23,12 @@ PASSES = I // 512
 QT = Q // P
 BT = B // P
 GROUPS = S * BT
-LEAD_MX = 5
-LEAD_RG = 11
-EARLY = 12
+UNITS = S * PASSES
+LEAD_MX = 6
+LEAD_RG = 12
+WEAVE = 2
+RAW_BUFS = 6
+FIN_LAG = 2
 
 TWO_PI_HI = 6.28125
 TWO_PI_LO = 2.0 * math.pi - 6.28125
@@ -37,18 +40,38 @@ def tile_quantumsuperposition_kernel(
 ):
     nc = tc.nc
     with ExitStack() as ctx:
+        ctx.enter_context(tc.manual_schedule())
         const = ctx.enter_context(tc.tile_pool(name="const", bufs=1))
         small = ctx.enter_context(tc.tile_pool(name="small", bufs=1))
-        raw_pool = ctx.enter_context(tc.tile_pool(name="raw", bufs=8))
+        raw_pool = ctx.enter_context(tc.tile_pool(name="raw", bufs=RAW_BUFS))
         wg_pool = ctx.enter_context(tc.tile_pool(name="wg", bufs=3))
-        code_pool = ctx.enter_context(tc.tile_pool(name="codes", bufs=4))
-        supt_pool = ctx.enter_context(tc.tile_pool(name="supt", bufs=2))
-        y_pool = ctx.enter_context(tc.tile_pool(name="y", bufs=6))
+        code_pool = ctx.enter_context(tc.tile_pool(name="codes", bufs=3))
+        supt_pool = ctx.enter_context(tc.tile_pool(name="supt", bufs=3))
+        y_pool = ctx.enter_context(tc.tile_pool(name="y", bufs=7))
         stat_pool = ctx.enter_context(tc.tile_pool(name="stat", bufs=4))
-        ps_acc = ctx.enter_context(tc.psum_pool(name="ps_acc", bufs=2))
+        ps_acc = ctx.enter_context(tc.psum_pool(name="ps_acc", bufs=3))
         ps_sup = ctx.enter_context(tc.psum_pool(name="ps_sup", bufs=4))
         ps_sum = ctx.enter_context(tc.psum_pool(name="ps_sum", bufs=1))
-        ps_beta = ctx.enter_context(tc.psum_pool(name="ps_beta", bufs=1))
+
+        par_a = small.tile([P, P], BF16, name="par_a")
+        par_b = small.tile([P, P], BF16, name="par_b")
+        gb_row = small.tile([P, 2 * Q], BF16, name="gb_row")
+        ones_bf = small.tile([P, P], BF16, name="ones_bf")
+        neghalf = const.tile([P, 1], F32, name="neghalf")
+        nc.vector.memset(par_b[64:128, :], 0.0)
+        nc.vector.memset(gb_row[:], 0.0)
+        nc.vector.memset(ones_bf[:], 1.0)
+        nc.vector.memset(neghalf[:], -0.5)
+        nc.scalar.dma_start(out=par_a[0:64, :], in_=amplitude_weights.rearrange("s (t q) -> (s t) q", q=P))
+        nc.scalar.dma_start(out=par_a[64:128, :], in_=phase_weights.rearrange("s (t q) -> (s t) q", q=P))
+        nc.scalar.dma_start(out=par_b[0:64, :], in_=b.rearrange("s (t q) -> (s t) q", q=P))
+        nc.scalar.dma_start(out=gb_row[0:1, 0:Q], in_=ln_gamma.rearrange("(o q) -> o q", o=1))
+        nc.scalar.dma_start(out=gb_row[0:1, Q : 2 * Q], in_=ln_beta.rearrange("(o q) -> o q", o=1))
+
+        x_sb = const.tile([P, BT * I], BF16, name="x_sb")
+        nc.sync.dma_start(
+            out=x_sb[:].rearrange("p (t k) -> p t k", t=BT), in_=language_features.rearrange("(t p) k -> p t k", p=P)
+        )
 
         raw = {}
 
@@ -60,65 +83,11 @@ def tile_quantumsuperposition_kernel(
             )
             raw[u] = t
 
-        load_unit(0)
-        x_sb = []
-        for bt in range(BT):
-            xt_sb = const.tile([P, I], BF16, name="x_sb%d" % bt)
-            nc.sync.dma_start(out=xt_sb[:], in_=language_features[bt * P : (bt + 1) * P, :])
-            x_sb.append(xt_sb)
-
-        par_a = small.tile([P, P], BF16, name="par_a")
-        par_b = small.tile([P, P], BF16, name="par_b")
-        beta_row = small.tile([P, Q], BF16, name="beta_row")
-        ones_bf = small.tile([P, P], BF16, name="ones_bf")
-        nc.vector.memset(par_b[64:128, :], 0.0)
-        nc.vector.memset(beta_row[:], 0.0)
-        nc.vector.memset(ones_bf[:], 1.0)
-        nc.scalar.dma_start(out=par_a[0:64, :], in_=amplitude_weights.rearrange("s (t q) -> (s t) q", q=P))
-        nc.scalar.dma_start(out=par_a[64:128, :], in_=phase_weights.rearrange("s (t q) -> (s t) q", q=P))
-        nc.scalar.dma_start(out=par_b[0:64, :], in_=b.rearrange("s (t q) -> (s t) q", q=P))
-        nc.scalar.dma_start(out=beta_row[0:1, :], in_=ln_beta.rearrange("(o q) -> o q", o=1))
-
-        for u in range(1, 4):
-            load_unit(u)
-        gamma_raw = small.tile([P, Q], BF16, name="gamma_raw")
-        nc.sync.dma_start(out=gamma_raw[:], in_=ln_gamma.partition_broadcast(P))
-        for u in range(4, 8):
+        for u in range(RAW_BUFS):
             load_unit(u)
 
         ident = const.tile([P, P], F32, name="ident")
         make_identity(nc, ident[:])
-        neghalf = const.tile([P, 1], F32, name="neghalf")
-        nc.vector.memset(neghalf[:], -0.5)
-        gamma_bc = const.tile([P, Q], BF16, name="gamma_bc")
-        nc.gpsimd.tensor_scalar(
-            out=gamma_bc[:], in0=gamma_raw[:], scalar1=math.sqrt(Q), scalar2=0.0, op0=ALU.mult, op1=ALU.add
-        )
-        beta_ps = ps_beta.tile([P, Q], BF16, name="beta_ps")
-        for h in range(2):
-            half = slice(h * 512, (h + 1) * 512)
-            nc.tensor.matmul(out=beta_ps[:, half], lhsT=ones_bf[:], rhs=beta_row[:, half], start=True, stop=True)
-
-        xc = const.tile([P, PASSES, B], U32, name="xc", align_bytes=64)
-        xs = const.tile([P, PASSES, B], U8, name="xs", align_bytes=64)
-        xw = [t[:].bitcast(F32).rearrange("p (g w u) -> p g u w", g=PASSES, u=2) for t in x_sb]
-        for g in range(PASSES):
-            xg = const.tile([P, 4 * B], BF16, name="xg%d" % g, align_bytes=64)
-            xg_words = xg[:].bitcast(F32).rearrange("p (r u) -> p r u", u=2)
-            for h in range(2):
-                xt = ps_sup.tile([P, 2, 256], F32, name="xt%d%d" % (g, h), tag="sup")
-                for bl in range(2):
-                    for u in range(2):
-                        nc.tensor.transpose(
-                            out=xt[:, u, bl * P : (bl + 1) * P], in_=xw[2 * h + bl][:, g, u, :], identity=ident[:]
-                        )
-                dst = xg_words[:, h * 256 : (h + 1) * 256, :]
-                src = xt[:].rearrange("p u r -> p r u")
-                if h == 0:
-                    nc.vector.tensor_copy(out=dst, in_=src)
-                else:
-                    nc.scalar.copy(out=dst, in_=src)
-            nc.vector.quantize_mx(out=xc[:, g, :].bitcast(FP8X4), scales=xs[:, g, :], in_=xg[:])
 
         par_af = small.tile([P, P], F32, name="par_af")
         par_bf = small.tile([P, P], F32, name="par_bf")
@@ -133,6 +102,23 @@ def tile_quantumsuperposition_kernel(
         pha_t = prm[:, 64:128]
         bias_t = prm[:, 128:192]
 
+        gamma_bc = const.tile([P, Q], BF16, name="gamma_bc")
+        beta_bc = const.tile([P, Q], BF16, name="beta_bc")
+        for k, dst_bc in enumerate((gamma_bc, beta_bc)):
+            gb_ps = ps_sup.tile([P, Q], BF16, name="gb_ps%d" % k, tag="sup")
+            for h in range(2):
+                nc.tensor.matmul(
+                    out=gb_ps[:, h * 512 : (h + 1) * 512],
+                    lhsT=ones_bf[:],
+                    rhs=gb_row[:, k * Q + h * 512 : k * Q + (h + 1) * 512],
+                    start=True,
+                    stop=True,
+                )
+            if k == 0:
+                nc.vector.tensor_copy(out=dst_bc[:], in_=gb_ps[:])
+            else:
+                nc.scalar.copy(out=dst_bc[:], in_=gb_ps[:])
+
         def st(ap):
             return ap.rearrange("p (s t) -> p s t", s=S)
 
@@ -146,12 +132,6 @@ def tile_quantumsuperposition_kernel(
         nc.vector.tensor_reduce(out=amax[:], in_=ts(amp_t), axis=AX.X, op=ALU.max)
         ash = small.tile([P, 64], F32, name="ash")
         nc.vector.tensor_tensor(out=st(ash[:]), in0=st(amp_t), in1=over_s(amax[:]), op=ALU.subtract)
-        aex = small.tile([P, 64], F32, name="aex")
-        nc.scalar.activation(out=aex[:], in_=ash[:], func=ACT.Exp)
-        asum = small.tile([P, QT], F32, name="asum")
-        nc.vector.tensor_reduce(out=asum[:], in_=ts(aex[:]), axis=AX.X, op=ALU.add)
-        arec = small.tile([P, QT], F32, name="arec")
-        nc.vector.reciprocal(out=arec[:], in_=asum[:])
 
         turns = small.tile([P, 64], F32, name="turns")
         nc.vector.tensor_scalar(
@@ -187,21 +167,55 @@ def tile_quantumsuperposition_kernel(
         nc.vector.tensor_scalar(
             out=ang5[:], in0=ang4[:], scalar1=-PI_BELOW, scalar2=PI_BELOW, op0=ALU.max, op1=ALU.min
         )
+
+        xc = const.tile([P, PASSES, B], U32, name="xc", align_bytes=64)
+        xs = const.tile([P, PASSES, B], U8, name="xs", align_bytes=64)
+        xw = x_sb[:].bitcast(F32).rearrange("p (t g w u) -> p t g u w", t=BT, g=PASSES, u=2)
+        xg = []
+        for g in range(PASSES):
+            xg_g = const.tile([P, 4 * B], BF16, name="xg%d" % g, align_bytes=64)
+            xg.append(xg_g)
+            xg_words = xg_g[:].bitcast(F32).rearrange("p (r u) -> p r u", u=2)
+            for h in range(2):
+                xt = ps_sup.tile([P, 2, 256], F32, name="xt%d%d" % (g, h), tag="sup")
+                for bl in range(2):
+                    for u in range(2):
+                        nc.tensor.transpose(
+                            out=xt[:, u, bl * P : (bl + 1) * P], in_=xw[:, 2 * h + bl, g, u, :], identity=ident[:]
+                        )
+                dst = xg_words[:, h * 256 : (h + 1) * 256, :]
+                src = xt[:].rearrange("p u r -> p r u")
+                if h == 0:
+                    nc.vector.tensor_copy(out=dst, in_=src)
+                else:
+                    nc.scalar.copy(out=dst, in_=src)
+        for g in range(PASSES):
+            nc.vector.quantize_mx(out=xc[:, g, :].bitcast(FP8X4), scales=xs[:, g, :], in_=xg[g][:])
+
+        aex = small.tile([P, 64], F32, name="aex")
+        nc.scalar.activation(out=aex[:], in_=ash[:], func=ACT.Exp)
         cosv = small.tile([P, 64], F32, name="cosv")
         nc.scalar.activation(out=cosv[:], in_=ang5[:], func=ACT.Sin)
-
-        ampl = small.tile([P, 64], F32, name="ampl")
-        nc.vector.tensor_tensor(out=st(ampl[:]), in0=st(aex[:]), in1=over_s(arec[:]), op=ALU.mult)
         mix_t = const.tile([P, 64], F32, name="mix_t")
-        nc.vector.tensor_tensor(out=mix_t[:], in0=ampl[:], in1=cosv[:], op=ALU.mult)
         bmix_t = const.tile([P, 64], F32, name="bmix_t")
-        nc.vector.tensor_tensor(out=bmix_t[:], in0=bias_t, in1=mix_t[:], op=ALU.mult)
+
+        def parameters_end():
+            asum = small.tile([P, QT], F32, name="asum")
+            nc.vector.tensor_reduce(out=asum[:], in_=ts(aex[:]), axis=AX.X, op=ALU.add)
+            arec = small.tile([P, QT], F32, name="arec")
+            nc.vector.reciprocal(out=arec[:], in_=asum[:])
+            ampl = small.tile([P, 64], F32, name="ampl")
+            nc.vector.tensor_tensor(out=st(ampl[:]), in0=st(aex[:]), in1=over_s(arec[:]), op=ALU.mult)
+            nc.vector.tensor_tensor(out=mix_t[:], in0=ampl[:], in1=cosv[:], op=ALU.mult)
+            nc.vector.tensor_tensor(out=bmix_t[:], in0=bias_t, in1=mix_t[:], op=ALU.mult)
 
         wg = {}
         wc = {}
         ws = {}
         supt = {}
+        acc = {}
         sup = {}
+        sums = {}
         ysb = {}
         negmean = {}
         varsum = {}
@@ -210,28 +224,19 @@ def tile_quantumsuperposition_kernel(
         def regroup(u, h):
             if h == 0:
                 wg[u] = wg_pool.tile([P, Q, 4], BF16, name="wg%d" % u, tag="wg", align_bytes=64)
-            g_cols, s_cols = (128, 192) if 2 * u + h < EARLY else (384, 128)
+            piece = 2 * u + h
+            v_cols = 248 if piece < 5 else (416 if piece < 11 else 304)
             lo = h * 512
-            m1 = lo + g_cols
-            m2 = m1 + s_cols
+            mid = lo + v_cols
             hi = lo + 512
-            nc.gpsimd.tensor_scalar(
-                out=wg[u][:, lo:m1, :],
-                in0=raw[u][:, :, lo:m1].rearrange("p t w -> p w t"),
-                scalar1=1.0,
-                scalar2=0.0,
-                op0=ALU.mult,
-                op1=ALU.add,
+            nc.vector.tensor_copy(
+                out=wg[u][:, lo:mid, :].rearrange("p (c i) t -> p c t i", i=4),
+                in_=raw[u][:, :, lo:mid].rearrange("p t (c i) -> p c t i", i=4),
             )
             nc.scalar.copy(
-                out=wg[u][:, m1:m2, :].rearrange("p (c i) t -> p c t i", i=4),
-                in_=raw[u][:, :, m1:m2].rearrange("p t (c i) -> p c t i", i=4),
+                out=wg[u][:, mid:hi, :].rearrange("p (c i) t -> p c t i", i=4),
+                in_=raw[u][:, :, mid:hi].rearrange("p t (c i) -> p c t i", i=4),
             )
-            if m2 < hi:
-                nc.vector.tensor_copy(
-                    out=wg[u][:, m2:hi, :].rearrange("p (c i) t -> p c t i", i=4),
-                    in_=raw[u][:, :, m2:hi].rearrange("p t (c i) -> p c t i", i=4),
-                )
 
         def quantise(u):
             s, c = divmod(u, PASSES)
@@ -244,50 +249,54 @@ def tile_quantumsuperposition_kernel(
                 in_=wg[u][:].rearrange("p w j -> p (w j)"),
             )
 
-        def states(s, qt):
+        def mx_pass(s, qt, c):
+            if c == 0:
+                acc[s, qt] = ps_acc.tile([P, B], F32, name="acc%d_%d" % (s, qt), tag="acc")
+            cols = slice(qt * P, (qt + 1) * P)
+            nc.tensor.matmul_mx(
+                out=acc[s, qt][:],
+                lhsT=wc[s][:, c, cols].bitcast(FP8X4),
+                lhsT_scale=ws[s][:, c, cols],
+                rhs=xc[:, c, :].bitcast(FP8X4),
+                rhs_scale=xs[:, c, :],
+                start=(c == 0),
+                stop=(c == PASSES - 1),
+            )
+
+        def mix_out(s, qt):
             if qt == 0:
                 supt[s] = supt_pool.tile([P, QT, B], F32, name="supt%d" % s, tag="supt")
-            cols = slice(qt * P, (qt + 1) * P)
-            acc = ps_acc.tile([P, B], F32, name="acc%d_%d" % (s, qt), tag="acc")
-            for c in range(PASSES):
-                nc.tensor.matmul_mx(
-                    out=acc[:],
-                    lhsT=wc[s][:, c, cols].bitcast(FP8X4),
-                    lhsT_scale=ws[s][:, c, cols],
-                    rhs=xc[:, c, :].bitcast(FP8X4),
-                    rhs_scale=xs[:, c, :],
-                    start=(c == 0),
-                    stop=(c == PASSES - 1),
-                )
             col = s * QT + qt
             nc.scalar.activation(
                 out=supt[s][:, qt, :],
-                in_=acc[:],
+                in_=acc[s, qt][:],
                 func=ACT.Identity,
                 scale=mix_t[:, col : col + 1],
                 bias=bmix_t[:, col : col + 1],
             )
 
-        sums = {}
-
-        def turn(n):
+        def turn_one(n, qt):
             s, bt = divmod(n, BT)
-            rows = slice(bt * P, (bt + 1) * P)
-            sup[n] = [ps_sup.tile([P, 512], F32, name="sup%d_%d" % (n, h), tag="sup") for h in range(2)]
-            sums[n] = ps_sum.tile([P, P], F32, name="sums%d" % n, tag="sums")
-            for qt in range(QT):
-                nc.tensor.transpose(
-                    out=sup[n][qt // 4][:, (qt % 4) * P : (qt % 4 + 1) * P], in_=supt[s][:, qt, rows], identity=ident[:]
-                )
-            for qt in range(QT):
-                nc.tensor.matmul(
-                    out=sums[n][:],
-                    lhsT=supt[s][:, qt, rows],
-                    rhs=ident[:],
-                    start=(qt == 0),
-                    stop=(qt == QT - 1),
-                    is_transpose=True,
-                )
+            if qt == 0:
+                sup[n] = [ps_sup.tile([P, 512], F32, name="sup%d_%d" % (n, h), tag="sup") for h in range(2)]
+            nc.tensor.transpose(
+                out=sup[n][qt // 4][:, (qt % 4) * P : (qt % 4 + 1) * P],
+                in_=supt[s][:, qt, bt * P : (bt + 1) * P],
+                identity=ident[:],
+            )
+
+        def turn_add(n, qt):
+            s, bt = divmod(n, BT)
+            if qt == 0:
+                sums[n] = ps_sum.tile([P, P], F32, name="sums%d" % n, tag="sums")
+            nc.tensor.matmul(
+                out=sums[n][:],
+                lhsT=supt[s][:, qt, bt * P : (bt + 1) * P],
+                rhs=ident[:],
+                start=(qt == 0),
+                stop=(qt == QT - 1),
+                is_transpose=True,
+            )
 
         def moments(n):
             junk = stat_pool.tile([P, P], F32, name="junk%d" % n, tag="junk")
@@ -320,42 +329,54 @@ def tile_quantumsuperposition_kernel(
 
         def inverse_std(n):
             tot = stat_pool.tile([P, 1], F32, name="tot%d" % n, tag="tot")
+            vare = stat_pool.tile([P, 1], F32, name="vare%d" % n, tag="vare")
             rstd[n] = stat_pool.tile([P, 1], F32, name="rstd%d" % n, tag="rstd")
+            nc.gpsimd.tensor_tensor(out=tot[:], in0=varsum[n][:, 0:1], in1=varsum[n][:, 1:2], op=ALU.add)
             nc.gpsimd.tensor_scalar(
-                out=tot[:],
-                in0=varsum[n][:, 0:1],
-                scalar1=varsum[n][:, 1:2],
-                scalar2=Q * LN_EPS,
-                op0=ALU.add,
-                op1=ALU.add,
+                out=vare[:], in0=tot[:], scalar1=1.0 / Q, scalar2=LN_EPS, op0=ALU.mult, op1=ALU.add
             )
-            nc.gpsimd.tensor_tensor(out=rstd[n][:], in0=tot[:], in1=neghalf[:], op=ALU.pow)
+            nc.gpsimd.tensor_tensor(out=rstd[n][:], in0=vare[:], in1=neghalf[:], op=ALU.pow)
 
         def finish(n):
             s, bt = divmod(n, BT)
             nc.vector.scalar_tensor_tensor(
-                out=ysb[n][:], in0=ysb[n][:], scalar=rstd[n][:], in1=beta_ps[:], op0=ALU.mult, op1=ALU.add
+                out=ysb[n][:], in0=ysb[n][:], scalar=rstd[n][:], in1=beta_bc[:], op0=ALU.mult, op1=ALU.add
             )
             nc.sync.dma_start(out=out[bt * P : (bt + 1) * P, s, :], in_=ysb[n][:])
 
-        for n in range(-LEAD_RG, GROUPS + 1):
-            if 0 <= n + 1 < GROUPS:
-                turn(n + 1)
+        for n in range(-LEAD_RG, GROUPS + FIN_LAG):
+            m = n + LEAD_MX
+            r = n + LEAD_RG
+            if 0 <= m - 1 < GROUPS:
+                mix_out((m - 1) // 4, 2 * ((m - 1) % 4) + 1)
             if 0 <= n < GROUPS:
                 moments(n)
-            if 0 <= n - 1:
-                finish(n - 1)
-            m = n + LEAD_MX
+
+            t_ops = []
+            if 0 <= n + 1 < GROUPS:
+                t_ops = [(turn_one, n + 1, qt) for qt in range(QT)] + [(turn_add, n + 1, qt) for qt in range(QT)]
+            m_ops = []
             if 0 <= m < GROUPS:
-                states(m // 4, 2 * (m % 4))
-                states(m // 4, 2 * (m % 4) + 1)
-            r = n + LEAD_RG
-            if r < 2 * S * PASSES:
+                m_ops = [(m // 4, 2 * (m % 4) + k // 2, k % 2) for k in range(4)]
+            runs = 4 // WEAVE
+            for k in range(runs):
+                for fn, g, qt in t_ops[k * 16 // runs : (k + 1) * 16 // runs]:
+                    fn(g, qt)
+                for s, qt, c in m_ops[k * WEAVE : (k + 1) * WEAVE]:
+                    mx_pass(s, qt, c)
+
+            if 0 <= n - FIN_LAG < GROUPS:
+                finish(n - FIN_LAG)
+            if r == 2:
+                parameters_end()
+            if r < 2 * UNITS:
                 regroup(r // 2, r % 2)
-                if r % 2 == 1 and r // 2 + 8 < S * PASSES:
-                    load_unit(r // 2 + 8)
-            if r >= 2 and r % 2 == 0 and r <= 2 * S * PASSES:
+                if r % 2 == 1 and r // 2 + RAW_BUFS < UNITS:
+                    load_unit(r // 2 + RAW_BUFS)
+            if r >= 2 and r % 2 == 0 and r <= 2 * UNITS:
                 quantise(r // 2 - 1)
+            if 0 <= m < GROUPS:
+                mix_out(m // 4, 2 * (m % 4))
             if 0 <= n < GROUPS:
                 centre(n)
                 inverse_std(n)

@@ -26,7 +26,6 @@ GROUPS = S * BT
 UNITS = S * PASSES
 LEAD_MX = 6
 LEAD_RG = 12
-WEAVE = 2
 RAW_BUFS = 6
 FIN_LAG = 2
 
@@ -68,10 +67,6 @@ def tile_quantumsuperposition_kernel(
         nc.scalar.dma_start(out=gb_row[0:1, 0:Q], in_=ln_gamma.rearrange("(o q) -> o q", o=1))
         nc.scalar.dma_start(out=gb_row[0:1, Q : 2 * Q], in_=ln_beta.rearrange("(o q) -> o q", o=1))
 
-        x_sb = const.tile([P, BT * I], BF16, name="x_sb")
-        nc.sync.dma_start(
-            out=x_sb[:].rearrange("p (t k) -> p t k", t=BT), in_=language_features.rearrange("(t p) k -> p t k", p=P)
-        )
 
         raw = {}
 
@@ -83,7 +78,12 @@ def tile_quantumsuperposition_kernel(
             )
             raw[u] = t
 
-        for u in range(RAW_BUFS):
+        load_unit(0)
+        x_sb = const.tile([P, BT * I], BF16, name="x_sb")
+        nc.sync.dma_start(
+            out=x_sb[:].rearrange("p (t k) -> p t k", t=BT), in_=language_features.rearrange("(t p) k -> p t k", p=P)
+        )
+        for u in range(1, RAW_BUFS):
             load_unit(u)
 
         ident = const.tile([P, P], F32, name="ident")
@@ -170,32 +170,34 @@ def tile_quantumsuperposition_kernel(
 
         xc = const.tile([P, PASSES, B], U32, name="xc", align_bytes=64)
         xs = const.tile([P, PASSES, B], U8, name="xs", align_bytes=64)
-        xw = x_sb[:].bitcast(F32).rearrange("p (t g w u) -> p t g u w", t=BT, g=PASSES, u=2)
-        xg = []
-        for g in range(PASSES):
-            xg_g = const.tile([P, 4 * B], BF16, name="xg%d" % g, align_bytes=64)
-            xg.append(xg_g)
-            xg_words = xg_g[:].bitcast(F32).rearrange("p (r u) -> p r u", u=2)
-            for h in range(2):
-                xt = ps_sup.tile([P, 2, 256], F32, name="xt%d%d" % (g, h), tag="sup")
-                for bl in range(2):
-                    for u in range(2):
-                        nc.tensor.transpose(
-                            out=xt[:, u, bl * P : (bl + 1) * P], in_=xw[:, 2 * h + bl, g, u, :], identity=ident[:]
-                        )
-                dst = xg_words[:, h * 256 : (h + 1) * 256, :]
-                src = xt[:].rearrange("p u r -> p r u")
-                if h == 0:
-                    nc.vector.tensor_copy(out=dst, in_=src)
-                else:
-                    nc.scalar.copy(out=dst, in_=src)
-        for g in range(PASSES):
-            nc.vector.quantize_mx(out=xc[:, g, :].bitcast(FP8X4), scales=xs[:, g, :], in_=xg[g][:])
-
         aex = small.tile([P, 64], F32, name="aex")
-        nc.scalar.activation(out=aex[:], in_=ash[:], func=ACT.Exp)
         cosv = small.tile([P, 64], F32, name="cosv")
-        nc.scalar.activation(out=cosv[:], in_=ang5[:], func=ACT.Sin)
+
+        def x_prepare():
+            xw = x_sb[:].bitcast(F32).rearrange("p (t g w u) -> p t g u w", t=BT, g=PASSES, u=2)
+            xg = []
+            for g in range(PASSES):
+                xg_g = const.tile([P, 4 * B], BF16, name="xg%d" % g, align_bytes=64)
+                xg.append(xg_g)
+                xg_words = xg_g[:].bitcast(F32).rearrange("p (r u) -> p r u", u=2)
+                for h in range(2):
+                    xt = ps_sup.tile([P, 2, 256], F32, name="xt%d%d" % (g, h), tag="sup")
+                    for bl in range(2):
+                        for u in range(2):
+                            nc.tensor.transpose(
+                                out=xt[:, u, bl * P : (bl + 1) * P], in_=xw[:, 2 * h + bl, g, u, :], identity=ident[:]
+                            )
+                    dst = xg_words[:, h * 256 : (h + 1) * 256, :]
+                    src = xt[:].rearrange("p u r -> p r u")
+                    if h == 0:
+                        nc.vector.tensor_copy(out=dst, in_=src)
+                    else:
+                        nc.scalar.copy(out=dst, in_=src)
+            for g in range(PASSES):
+                nc.vector.quantize_mx(out=xc[:, g, :].bitcast(FP8X4), scales=xs[:, g, :], in_=xg[g][:])
+
+            nc.scalar.activation(out=aex[:], in_=ash[:], func=ACT.Exp)
+            nc.scalar.activation(out=cosv[:], in_=ang5[:], func=ACT.Sin)
         mix_t = const.tile([P, 64], F32, name="mix_t")
         bmix_t = const.tile([P, 64], F32, name="bmix_t")
 
@@ -298,14 +300,16 @@ def tile_quantumsuperposition_kernel(
                 is_transpose=True,
             )
 
-        def moments(n):
+        def mean_of(n):
             junk = stat_pool.tile([P, P], F32, name="junk%d" % n, tag="junk")
             negmean[n] = stat_pool.tile([P, 1], F32, name="negmean%d" % n, tag="negmean")
-            varsum[n] = stat_pool.tile([P, 2], F32, name="varsum%d" % n, tag="varsum")
-            ysb[n] = y_pool.tile([P, Q], F32, name="y%d" % n, tag="y")
             nc.scalar.activation(
                 out=junk[:], in_=sums[n][:], func=ACT.Copy, scale=-1.0 / Q, accum_out=negmean[n][:]
             )
+
+        def squares(n):
+            varsum[n] = stat_pool.tile([P, 2], F32, name="varsum%d" % n, tag="varsum")
+            ysb[n] = y_pool.tile([P, Q], F32, name="y%d" % n, tag="y")
             for h in range(2):
                 nc.scalar.activation(
                     out=ysb[n][:, h * 512 : (h + 1) * 512],
@@ -347,27 +351,31 @@ def tile_quantumsuperposition_kernel(
         for n in range(-LEAD_RG, GROUPS + FIN_LAG):
             m = n + LEAD_MX
             r = n + LEAD_RG
+            nxt = n + 1
+            if 0 <= n < GROUPS:
+                squares(n)
             if 0 <= m - 1 < GROUPS:
                 mix_out((m - 1) // 4, 2 * ((m - 1) % 4) + 1)
-            if 0 <= n < GROUPS:
-                moments(n)
 
-            t_ops = []
-            if 0 <= n + 1 < GROUPS:
-                t_ops = [(turn_one, n + 1, qt) for qt in range(QT)] + [(turn_add, n + 1, qt) for qt in range(QT)]
-            m_ops = []
+            if 0 <= nxt < GROUPS:
+                for qt in range(QT):
+                    turn_add(nxt, qt)
             if 0 <= m < GROUPS:
-                m_ops = [(m // 4, 2 * (m % 4) + k // 2, k % 2) for k in range(4)]
-            runs = 4 // WEAVE
-            for k in range(runs):
-                for fn, g, qt in t_ops[k * 16 // runs : (k + 1) * 16 // runs]:
-                    fn(g, qt)
-                for s, qt, c in m_ops[k * WEAVE : (k + 1) * WEAVE]:
-                    mx_pass(s, qt, c)
+                for c in range(PASSES):
+                    mx_pass(m // 4, 2 * (m % 4), c)
+            if 0 <= nxt < GROUPS:
+                mean_of(nxt)
+                for qt in range(QT):
+                    turn_one(nxt, qt)
+            if 0 <= m < GROUPS:
+                for c in range(PASSES):
+                    mx_pass(m // 4, 2 * (m % 4) + 1, c)
 
             if 0 <= n - FIN_LAG < GROUPS:
                 finish(n - FIN_LAG)
             if r == 2:
+                x_prepare()
+            if r == 4:
                 parameters_end()
             if r < 2 * UNITS:
                 regroup(r // 2, r % 2)

@@ -48,9 +48,10 @@ def tile_quantumsuperposition_kernel(
         supt_pool = ctx.enter_context(tc.tile_pool(name="supt", bufs=3))
         y_pool = ctx.enter_context(tc.tile_pool(name="y", bufs=7))
         stat_pool = ctx.enter_context(tc.tile_pool(name="stat", bufs=4))
-        ps_acc = ctx.enter_context(tc.psum_pool(name="ps_acc", bufs=3))
+        ps_acc = ctx.enter_context(tc.psum_pool(name="ps_acc", bufs=2))
         ps_sup = ctx.enter_context(tc.psum_pool(name="ps_sup", bufs=4))
         ps_sum = ctx.enter_context(tc.psum_pool(name="ps_sum", bufs=1))
+        ps_beta = ctx.enter_context(tc.psum_pool(name="ps_beta", bufs=1))
 
         par_a = small.tile([P, P], BF16, name="par_a")
         par_b = small.tile([P, P], BF16, name="par_b")
@@ -103,21 +104,18 @@ def tile_quantumsuperposition_kernel(
         bias_t = prm[:, 128:192]
 
         gamma_bc = const.tile([P, Q], BF16, name="gamma_bc")
-        beta_bc = const.tile([P, Q], BF16, name="beta_bc")
-        for k, dst_bc in enumerate((gamma_bc, beta_bc)):
-            gb_ps = ps_sup.tile([P, Q], BF16, name="gb_ps%d" % k, tag="sup")
+        gamma_ps = ps_sup.tile([P, Q], BF16, name="gamma_ps", tag="sup")
+        beta_ps = ps_beta.tile([P, Q], BF16, name="beta_ps")
+        for k, dst_ps in enumerate((gamma_ps, beta_ps)):
             for h in range(2):
                 nc.tensor.matmul(
-                    out=gb_ps[:, h * 512 : (h + 1) * 512],
+                    out=dst_ps[:, h * 512 : (h + 1) * 512],
                     lhsT=ones_bf[:],
                     rhs=gb_row[:, k * Q + h * 512 : k * Q + (h + 1) * 512],
                     start=True,
                     stop=True,
                 )
-            if k == 0:
-                nc.vector.tensor_copy(out=dst_bc[:], in_=gb_ps[:])
-            else:
-                nc.scalar.copy(out=dst_bc[:], in_=gb_ps[:])
+        nc.vector.tensor_scalar(out=gamma_bc[:], in0=gamma_ps[:], scalar1=math.sqrt(Q), scalar2=None, op0=ALU.mult)
 
         def st(ap):
             return ap.rearrange("p (s t) -> p s t", s=S)
@@ -223,21 +221,43 @@ def tile_quantumsuperposition_kernel(
         varsum = {}
         rstd = {}
 
+        def shares(piece):
+            if piece < 5:
+                return 0, 264
+            if piece < 11:
+                return 0, 96
+            return 224, 176
+
         def regroup(u, h):
             if h == 0:
                 wg[u] = wg_pool.tile([P, Q, 4], BF16, name="wg%d" % u, tag="wg", align_bytes=64)
-            piece = 2 * u + h
-            v_cols = 248 if piece < 5 else (416 if piece < 11 else 304)
-            lo = h * 512
-            mid = lo + v_cols
-            hi = lo + 512
-            nc.vector.tensor_copy(
+            g_cols, s_cols = shares(2 * u + h)
+            lo = h * 512 + g_cols
+            mid = lo + s_cols
+            hi = (h + 1) * 512
+            nc.scalar.copy(
                 out=wg[u][:, lo:mid, :].rearrange("p (c i) t -> p c t i", i=4),
                 in_=raw[u][:, :, lo:mid].rearrange("p t (c i) -> p c t i", i=4),
             )
-            nc.scalar.copy(
+            nc.vector.tensor_copy(
                 out=wg[u][:, mid:hi, :].rearrange("p (c i) t -> p c t i", i=4),
                 in_=raw[u][:, :, mid:hi].rearrange("p t (c i) -> p c t i", i=4),
+            )
+
+        def regroup_gpsimd(u, h):
+            g_cols, s_cols = shares(2 * u + h)
+            if g_cols == 0:
+                return
+            one = stat_pool.tile([P, 1], F32, name="one%d_%d" % (u, h), tag="one")
+            nc.vector.memset(one[:], 1.0)
+            lo = h * 512
+            nc.gpsimd.tensor_scalar(
+                out=wg[u][:, lo : lo + g_cols, :],
+                in0=raw[u][:, :, lo : lo + g_cols].rearrange("p t w -> p w t"),
+                scalar1=one[:],
+                scalar2=0.0,
+                op0=ALU.mult,
+                op1=ALU.add,
             )
 
         def quantise(u):
@@ -333,18 +353,21 @@ def tile_quantumsuperposition_kernel(
 
         def inverse_std(n):
             tot = stat_pool.tile([P, 1], F32, name="tot%d" % n, tag="tot")
-            vare = stat_pool.tile([P, 1], F32, name="vare%d" % n, tag="vare")
             rstd[n] = stat_pool.tile([P, 1], F32, name="rstd%d" % n, tag="rstd")
-            nc.gpsimd.tensor_tensor(out=tot[:], in0=varsum[n][:, 0:1], in1=varsum[n][:, 1:2], op=ALU.add)
             nc.gpsimd.tensor_scalar(
-                out=vare[:], in0=tot[:], scalar1=1.0 / Q, scalar2=LN_EPS, op0=ALU.mult, op1=ALU.add
+                out=tot[:],
+                in0=varsum[n][:, 0:1],
+                scalar1=varsum[n][:, 1:2],
+                scalar2=Q * LN_EPS,
+                op0=ALU.add,
+                op1=ALU.add,
             )
-            nc.gpsimd.tensor_tensor(out=rstd[n][:], in0=vare[:], in1=neghalf[:], op=ALU.pow)
+            nc.gpsimd.tensor_tensor(out=rstd[n][:], in0=tot[:], in1=neghalf[:], op=ALU.pow)
 
         def finish(n):
             s, bt = divmod(n, BT)
             nc.vector.scalar_tensor_tensor(
-                out=ysb[n][:], in0=ysb[n][:], scalar=rstd[n][:], in1=beta_bc[:], op0=ALU.mult, op1=ALU.add
+                out=ysb[n][:], in0=ysb[n][:], scalar=rstd[n][:], in1=beta_ps[:], op0=ALU.mult, op1=ALU.add
             )
             nc.sync.dma_start(out=out[bt * P : (bt + 1) * P, s, :], in_=ysb[n][:])
 
@@ -371,20 +394,22 @@ def tile_quantumsuperposition_kernel(
                 for c in range(PASSES):
                     mx_pass(m // 4, 2 * (m % 4) + 1, c)
 
-            if 0 <= n - FIN_LAG < GROUPS:
-                finish(n - FIN_LAG)
             if r == 2:
                 x_prepare()
             if r == 4:
                 parameters_end()
             if r < 2 * UNITS:
                 regroup(r // 2, r % 2)
-                if r % 2 == 1 and r // 2 + RAW_BUFS < UNITS:
-                    load_unit(r // 2 + RAW_BUFS)
             if r >= 2 and r % 2 == 0 and r <= 2 * UNITS:
                 quantise(r // 2 - 1)
+            if r < 2 * UNITS:
+                regroup_gpsimd(r // 2, r % 2)
+                if r % 2 == 1 and r // 2 + RAW_BUFS < UNITS:
+                    load_unit(r // 2 + RAW_BUFS)
             if 0 <= m < GROUPS:
                 mix_out(m // 4, 2 * (m % 4))
             if 0 <= n < GROUPS:
                 centre(n)
                 inverse_std(n)
+            if 0 <= n - FIN_LAG < GROUPS:
+                finish(n - FIN_LAG)

@@ -28,6 +28,7 @@ LEAD_MX = 6
 LEAD_RG = 12
 RAW_BUFS = 6
 FIN_LAG = 2
+G_LEAD = 2
 
 TWO_PI_HI = 6.28125
 TWO_PI_LO = 2.0 * math.pi - 6.28125
@@ -43,7 +44,7 @@ def tile_quantumsuperposition_kernel(
         const = ctx.enter_context(tc.tile_pool(name="const", bufs=1))
         small = ctx.enter_context(tc.tile_pool(name="small", bufs=1))
         raw_pool = ctx.enter_context(tc.tile_pool(name="raw", bufs=RAW_BUFS))
-        wg_pool = ctx.enter_context(tc.tile_pool(name="wg", bufs=3))
+        wg_pool = ctx.enter_context(tc.tile_pool(name="wg", bufs=4))
         code_pool = ctx.enter_context(tc.tile_pool(name="codes", bufs=3))
         supt_pool = ctx.enter_context(tc.tile_pool(name="supt", bufs=3))
         y_pool = ctx.enter_context(tc.tile_pool(name="y", bufs=7))
@@ -228,9 +229,13 @@ def tile_quantumsuperposition_kernel(
                 return 0, 96
             return 224, 176
 
-        def regroup(u, h):
-            if h == 0:
+        def grouped(u):
+            if u not in wg:
                 wg[u] = wg_pool.tile([P, Q, 4], BF16, name="wg%d" % u, tag="wg", align_bytes=64)
+            return wg[u]
+
+        def regroup(u, h):
+            grouped(u)
             g_cols, s_cols = shares(2 * u + h)
             lo = h * 512 + g_cols
             mid = lo + s_cols
@@ -248,6 +253,7 @@ def tile_quantumsuperposition_kernel(
             g_cols, s_cols = shares(2 * u + h)
             if g_cols == 0:
                 return
+            grouped(u)
             one = stat_pool.tile([P, 1], F32, name="one%d_%d" % (u, h), tag="one")
             nc.vector.memset(one[:], 1.0)
             lo = h * 512
@@ -400,12 +406,13 @@ def tile_quantumsuperposition_kernel(
                 parameters_end()
             if r < 2 * UNITS:
                 regroup(r // 2, r % 2)
-            if r >= 2 and r % 2 == 0 and r <= 2 * UNITS:
-                quantise(r // 2 - 1)
-            if r < 2 * UNITS:
-                regroup_gpsimd(r // 2, r % 2)
                 if r % 2 == 1 and r // 2 + RAW_BUFS < UNITS:
                     load_unit(r // 2 + RAW_BUFS)
+            if r >= 2 and r % 2 == 0 and r <= 2 * UNITS:
+                quantise(r // 2 - 1)
+            ahead = r + G_LEAD
+            if ahead < 2 * UNITS:
+                regroup_gpsimd(ahead // 2, ahead % 2)
             if 0 <= m < GROUPS:
                 mix_out(m // 4, 2 * (m % 4))
             if 0 <= n < GROUPS:

@@ -28,7 +28,6 @@ LEAD_MX = 6
 LEAD_RG = 12
 RAW_BUFS = 6
 FIN_LAG = 2
-G_LEAD = 2
 
 TWO_PI_HI = 6.28125
 TWO_PI_LO = 2.0 * math.pi - 6.28125
@@ -44,7 +43,7 @@ def tile_quantumsuperposition_kernel(
         const = ctx.enter_context(tc.tile_pool(name="const", bufs=1))
         small = ctx.enter_context(tc.tile_pool(name="small", bufs=1))
         raw_pool = ctx.enter_context(tc.tile_pool(name="raw", bufs=RAW_BUFS))
-        wg_pool = ctx.enter_context(tc.tile_pool(name="wg", bufs=4))
+        wg_pool = ctx.enter_context(tc.tile_pool(name="wg", bufs=3))
         code_pool = ctx.enter_context(tc.tile_pool(name="codes", bufs=3))
         supt_pool = ctx.enter_context(tc.tile_pool(name="supt", bufs=3))
         y_pool = ctx.enter_context(tc.tile_pool(name="y", bufs=7))
@@ -227,15 +226,11 @@ def tile_quantumsuperposition_kernel(
                 return 0, 264
             if piece < 11:
                 return 0, 96
-            return 224, 176
-
-        def grouped(u):
-            if u not in wg:
-                wg[u] = wg_pool.tile([P, Q, 4], BF16, name="wg%d" % u, tag="wg", align_bytes=64)
-            return wg[u]
+            return 224, 136
 
         def regroup(u, h):
-            grouped(u)
+            if h == 0:
+                wg[u] = wg_pool.tile([P, Q, 4], BF16, name="wg%d" % u, tag="wg", align_bytes=64)
             g_cols, s_cols = shares(2 * u + h)
             lo = h * 512 + g_cols
             mid = lo + s_cols
@@ -253,7 +248,6 @@ def tile_quantumsuperposition_kernel(
             g_cols, s_cols = shares(2 * u + h)
             if g_cols == 0:
                 return
-            grouped(u)
             one = stat_pool.tile([P, 1], F32, name="one%d_%d" % (u, h), tag="one")
             nc.vector.memset(one[:], 1.0)
             lo = h * 512
@@ -406,13 +400,12 @@ def tile_quantumsuperposition_kernel(
                 parameters_end()
             if r < 2 * UNITS:
                 regroup(r // 2, r % 2)
-                if r % 2 == 1 and r // 2 + RAW_BUFS < UNITS:
-                    load_unit(r // 2 + RAW_BUFS)
             if r >= 2 and r % 2 == 0 and r <= 2 * UNITS:
                 quantise(r // 2 - 1)
-            ahead = r + G_LEAD
-            if ahead < 2 * UNITS:
-                regroup_gpsimd(ahead // 2, ahead % 2)
+            if r < 2 * UNITS:
+                regroup_gpsimd(r // 2, r % 2)
+                if r % 2 == 1 and r // 2 + RAW_BUFS < UNITS:
+                    load_unit(r // 2 + RAW_BUFS)
             if 0 <= m < GROUPS:
                 mix_out(m // 4, 2 * (m % 4))
             if 0 <= n < GROUPS:

@@ -74,9 +74,12 @@ def tile_quantumsuperposition_kernel(
         def load_unit(u):
             s, c = divmod(u, PASSES)
             t = raw_pool.tile([P, 4, Q], BF16, name="raw%d" % u, tag="raw")
-            nc.sync.dma_start(
-                out=t[:], in_=W[s, c * 512 : (c + 1) * 512, :].rearrange("(p j) q -> p j q", j=4)
-            )
+            rows = W[s, c * 512 : (c + 1) * 512, :].rearrange("(p j) q -> p j q", j=4)
+            if u == 0:
+                for h in range(2):
+                    nc.sync.dma_start(out=t[:, :, h * 512 : (h + 1) * 512], in_=rows[:, :, h * 512 : (h + 1) * 512])
+            else:
+                nc.sync.dma_start(out=t[:], in_=rows)
             raw[u] = t
 
         load_unit(0)

@@ -27,7 +27,7 @@ UNITS = S * PASSES
 LEAD_MX = 6
 LEAD_RG = 12
 RAW_BUFS = 6
-FIN_LAG = 2
+FIN_LAG = 1
 
 TWO_PI_HI = 6.28125
 TWO_PI_LO = 2.0 * math.pi - 6.28125

@@ -58,16 +58,15 @@ def tile_quantumsuperposition_kernel(
         gb_row = small.tile([P, 2 * Q], BF16, name="gb_row")
         ones_bf = small.tile([P, P], BF16, name="ones_bf")
         neghalf = const.tile([P, 1], F32, name="neghalf")
-        nc.vector.memset(par_b[64:128, :], 0.0)
-        nc.vector.memset(gb_row[:], 0.0)
-        nc.vector.memset(ones_bf[:], 1.0)
         nc.vector.memset(neghalf[:], -0.5)
+        nc.vector.memset(par_b[64:128, :], 0.0)
+        nc.vector.memset(ones_bf[:], 1.0)
+        nc.vector.memset(gb_row[:], 0.0)
         nc.scalar.dma_start(out=par_a[0:64, :], in_=amplitude_weights.rearrange("s (t q) -> (s t) q", q=P))
         nc.scalar.dma_start(out=par_a[64:128, :], in_=phase_weights.rearrange("s (t q) -> (s t) q", q=P))
-        nc.scalar.dma_start(out=par_b[0:64, :], in_=b.rearrange("s (t q) -> (s t) q", q=P))
-        nc.scalar.dma_start(out=gb_row[0:1, 0:Q], in_=ln_gamma.rearrange("(o q) -> o q", o=1))
-        nc.scalar.dma_start(out=gb_row[0:1, Q : 2 * Q], in_=ln_beta.rearrange("(o q) -> o q", o=1))
-
+        nc.sync.dma_start(out=par_b[0:64, :], in_=b.rearrange("s (t q) -> (s t) q", q=P))
+        warm = small.tile([P, 1], F32, name="warm")
+        nc.scalar.activation(out=warm[:], in_=neghalf[:], func=ACT.Exp)
 
         raw = {}
 
@@ -87,38 +86,22 @@ def tile_quantumsuperposition_kernel(
         nc.sync.dma_start(
             out=x_sb[:].rearrange("p (t k) -> p t k", t=BT), in_=language_features.rearrange("(t p) k -> p t k", p=P)
         )
+        nc.sync.dma_start(out=gb_row[0:1, 0:Q], in_=ln_gamma.rearrange("(o q) -> o q", o=1))
+        nc.sync.dma_start(out=gb_row[0:1, Q : 2 * Q], in_=ln_beta.rearrange("(o q) -> o q", o=1))
         for u in range(1, RAW_BUFS):
             load_unit(u)
 
         ident = const.tile([P, P], F32, name="ident")
         make_identity(nc, ident[:])
+        ident_bf = const.tile([P, P], BF16, name="ident_bf")
+        nc.vector.tensor_copy(out=ident_bf[:], in_=ident[:])
 
-        par_af = small.tile([P, P], F32, name="par_af")
-        par_bf = small.tile([P, P], F32, name="par_bf")
-        nc.vector.tensor_copy(out=par_af[:], in_=par_a[:])
-        nc.vector.tensor_copy(out=par_bf[:], in_=par_b[:])
-        par_ps = ps_acc.tile([P, 512], F32, name="par_ps", tag="acc")
-        nc.tensor.transpose(out=par_ps[:, 0:P], in_=par_af[:], identity=ident[:])
-        nc.tensor.transpose(out=par_ps[:, P : 2 * P], in_=par_bf[:], identity=ident[:])
         prm = small.tile([P, 192], F32, name="prm")
-        nc.vector.tensor_copy(out=prm[:], in_=par_ps[:, 0:192])
         amp_t = prm[:, 0:64]
         pha_t = prm[:, 64:128]
         bias_t = prm[:, 128:192]
-
-        gamma_bc = const.tile([P, Q], BF16, name="gamma_bc")
-        gamma_ps = ps_sup.tile([P, Q], BF16, name="gamma_ps", tag="sup")
-        beta_ps = ps_beta.tile([P, Q], BF16, name="beta_ps")
-        for k, dst_ps in enumerate((gamma_ps, beta_ps)):
-            for h in range(2):
-                nc.tensor.matmul(
-                    out=dst_ps[:, h * 512 : (h + 1) * 512],
-                    lhsT=ones_bf[:],
-                    rhs=gb_row[:, k * Q + h * 512 : k * Q + (h + 1) * 512],
-                    start=True,
-                    stop=True,
-                )
-        nc.vector.tensor_scalar(out=gamma_bc[:], in0=gamma_ps[:], scalar1=math.sqrt(Q), scalar2=None, op0=ALU.mult)
+        ash = small.tile([P, 64], F32, name="ash")
+        ang_clip = small.tile([P, 64], F32, name="ang_clip")
 
         def st(ap):
             return ap.rearrange("p (s t) -> p s t", s=S)
@@ -129,45 +112,52 @@ def tile_quantumsuperposition_kernel(
         def over_s(ap):
             return ap.unsqueeze(1).to_broadcast([P, S, QT])
 
-        amax = small.tile([P, QT], F32, name="amax")
-        nc.vector.tensor_reduce(out=amax[:], in_=ts(amp_t), axis=AX.X, op=ALU.max)
-        ash = small.tile([P, 64], F32, name="ash")
-        nc.vector.tensor_tensor(out=st(ash[:]), in0=st(amp_t), in1=over_s(amax[:]), op=ALU.subtract)
+        def parameters_begin():
+            par_ps = ps_acc.tile([P, 2 * P], BF16, name="par_ps", tag="acc")
+            nc.tensor.transpose(out=par_ps[:, 0:P], in_=par_a[:], identity=ident_bf[:])
+            nc.tensor.transpose(out=par_ps[:, P : 2 * P], in_=par_b[:], identity=ident_bf[:])
+            nc.vector.tensor_copy(out=prm[:], in_=par_ps[:, 0:192])
 
-        turns = small.tile([P, 64], F32, name="turns")
-        nc.vector.tensor_scalar(
-            out=turns[:], in0=pha_t, scalar1=1.0 / (2.0 * math.pi), scalar2=0.25, op0=ALU.mult, op1=ALU.add
-        )
-        turns_i = small.tile([P, 64], I32, name="turns_i")
-        nc.vector.tensor_copy(out=turns_i[:], in_=turns[:])
-        turns_f = small.tile([P, 64], F32, name="turns_f")
-        nc.vector.tensor_copy(out=turns_f[:], in_=turns_i[:])
-        ang0 = small.tile([P, 64], F32, name="ang0")
-        nc.vector.tensor_scalar(out=ang0[:], in0=pha_t, scalar1=0.5 * math.pi, scalar2=None, op0=ALU.add)
-        ang1 = small.tile([P, 64], F32, name="ang1")
-        nc.vector.scalar_tensor_tensor(
-            out=ang1[:], in0=turns_f[:], scalar=-TWO_PI_HI, in1=ang0[:], op0=ALU.mult, op1=ALU.add
-        )
-        ang2 = small.tile([P, 64], F32, name="ang2")
-        nc.vector.scalar_tensor_tensor(
-            out=ang2[:], in0=turns_f[:], scalar=-TWO_PI_LO, in1=ang1[:], op0=ALU.mult, op1=ALU.add
-        )
-        fix1 = small.tile([P, 64], F32, name="fix1")
-        nc.vector.tensor_scalar(
-            out=fix1[:], in0=ang2[:], scalar1=math.pi, scalar2=-2.0 * math.pi, op0=ALU.is_gt, op1=ALU.mult
-        )
-        ang3 = small.tile([P, 64], F32, name="ang3")
-        nc.vector.tensor_tensor(out=ang3[:], in0=ang2[:], in1=fix1[:], op=ALU.add)
-        fix2 = small.tile([P, 64], F32, name="fix2")
-        nc.vector.tensor_scalar(
-            out=fix2[:], in0=ang3[:], scalar1=-math.pi, scalar2=2.0 * math.pi, op0=ALU.is_lt, op1=ALU.mult
-        )
-        ang4 = small.tile([P, 64], F32, name="ang4")
-        nc.vector.tensor_tensor(out=ang4[:], in0=ang3[:], in1=fix2[:], op=ALU.add)
-        ang5 = small.tile([P, 64], F32, name="ang5")
-        nc.vector.tensor_scalar(
-            out=ang5[:], in0=ang4[:], scalar1=-PI_BELOW, scalar2=PI_BELOW, op0=ALU.max, op1=ALU.min
-        )
+            turns = small.tile([P, 64], F32, name="turns")
+            nc.vector.tensor_scalar(
+                out=turns[:], in0=pha_t, scalar1=1.0 / (2.0 * math.pi), scalar2=0.25, op0=ALU.mult, op1=ALU.add
+            )
+            amax = small.tile([P, QT], F32, name="amax")
+            nc.vector.tensor_reduce(out=amax[:], in_=ts(amp_t), axis=AX.X, op=ALU.max)
+            turns_i = small.tile([P, 64], I32, name="turns_i")
+            nc.vector.tensor_copy(out=turns_i[:], in_=turns[:])
+            nc.vector.tensor_tensor(out=st(ash[:]), in0=st(amp_t), in1=over_s(amax[:]), op=ALU.subtract)
+            turns_f = small.tile([P, 64], F32, name="turns_f")
+            nc.vector.tensor_copy(out=turns_f[:], in_=turns_i[:])
+            ang0 = small.tile([P, 64], F32, name="ang0")
+            nc.vector.tensor_scalar(out=ang0[:], in0=pha_t, scalar1=0.5 * math.pi, scalar2=None, op0=ALU.add)
+            ang1 = small.tile([P, 64], F32, name="ang1")
+            nc.vector.scalar_tensor_tensor(
+                out=ang1[:], in0=turns_f[:], scalar=-TWO_PI_HI, in1=ang0[:], op0=ALU.mult, op1=ALU.add
+            )
+            ang2 = small.tile([P, 64], F32, name="ang2")
+            nc.vector.scalar_tensor_tensor(
+                out=ang2[:], in0=turns_f[:], scalar=-TWO_PI_LO, in1=ang1[:], op0=ALU.mult, op1=ALU.add
+            )
+            nc.vector.tensor_scalar(
+                out=ang_clip[:], in0=ang2[:], scalar1=-PI_BELOW, scalar2=PI_BELOW, op0=ALU.max, op1=ALU.min
+            )
+
+        gamma_bc = const.tile([P, Q], BF16, name="gamma_bc")
+        beta_ps = ps_beta.tile([P, Q], BF16, name="beta_ps")
+
+        def gamma_beta_spread():
+            gamma_ps = ps_sup.tile([P, Q], BF16, name="gamma_ps", tag="sup")
+            for k, dst_ps in enumerate((gamma_ps, beta_ps)):
+                for h in range(2):
+                    nc.tensor.matmul(
+                        out=dst_ps[:, h * 512 : (h + 1) * 512],
+                        lhsT=ones_bf[:],
+                        rhs=gb_row[:, k * Q + h * 512 : k * Q + (h + 1) * 512],
+                        start=True,
+                        stop=True,
+                    )
+            return gamma_ps
 
         xc = const.tile([P, PASSES, B], U32, name="xc", align_bytes=64)
         xs = const.tile([P, PASSES, B], U8, name="xs", align_bytes=64)
@@ -194,11 +184,15 @@ def tile_quantumsuperposition_kernel(
                         nc.vector.tensor_copy(out=dst, in_=src)
                     else:
                         nc.scalar.copy(out=dst, in_=src)
+            return xg
+
+        def x_quantise(xg):
             for g in range(PASSES):
                 nc.vector.quantize_mx(out=xc[:, g, :].bitcast(FP8X4), scales=xs[:, g, :], in_=xg[g][:])
 
+        def parameters_middle():
             nc.scalar.activation(out=aex[:], in_=ash[:], func=ACT.Exp)
-            nc.scalar.activation(out=cosv[:], in_=ang5[:], func=ACT.Sin)
+            nc.scalar.activation(out=cosv[:], in_=ang_clip[:], func=ACT.Sin)
         mix_t = const.tile([P, 64], F32, name="mix_t")
         bmix_t = const.tile([P, 64], F32, name="bmix_t")
 
@@ -398,11 +392,20 @@ def tile_quantumsuperposition_kernel(
                     mx_pass(m // 4, 2 * (m % 4) + 1, c)
 
             if r == 2:
-                x_prepare()
-            if r == 4:
-                parameters_end()
+                parameters_begin()
+                parameters_middle()
+                x_grouped = x_prepare()
+                gamma_ps = gamma_beta_spread()
+            if r == 6:
+                nc.vector.tensor_scalar(
+                    out=gamma_bc[:], in0=gamma_ps[:], scalar1=math.sqrt(Q), scalar2=None, op0=ALU.mult
+                )
             if r < 2 * UNITS:
                 regroup(r // 2, r % 2)
+            if r == 3:
+                x_quantise(x_grouped)
+            if r == 4:
+                parameters_end()
             if r >= 2 and r % 2 == 0 and r <= 2 * UNITS:
                 quantise(r // 2 - 1)
             if r < 2 * UNITS:

@@ -26,8 +26,10 @@ GROUPS = S * BT
 UNITS = S * PASSES
 LEAD_MX = 6
 LEAD_RG = 12
+FIRST_WIDE = 6
+GPS_COLS = 592
+SCA_COLS = 240
 RAW_BUFS = 6
-FIN_LAG = 1
 
 TWO_PI_HI = 6.28125
 TWO_PI_LO = 2.0 * math.pi - 6.28125
@@ -216,6 +218,7 @@ def tile_quantumsuperposition_kernel(
         ysb = {}
         negmean = {}
         varsum = {}
+        tot = {}
         rstd = {}
 
         def shares(piece):
@@ -256,6 +259,37 @@ def tile_quantumsuperposition_kernel(
                 op0=ALU.mult,
                 op1=ALU.add,
             )
+
+        def regroup_wide_vector(u):
+            wg[u] = wg_pool.tile([P, Q, 4], BF16, name="wg%d" % u, tag="wg", align_bytes=64)
+            lo = GPS_COLS + SCA_COLS
+            nc.vector.tensor_copy(
+                out=wg[u][:, lo:Q, :].rearrange("p (c i) t -> p c t i", i=4),
+                in_=raw[u][:, :, lo:Q].rearrange("p t (c i) -> p c t i", i=4),
+            )
+
+        def regroup_wide_scalar(u, h):
+            lo = GPS_COLS + h * (SCA_COLS // 2)
+            hi = lo + SCA_COLS // 2
+            nc.scalar.copy(
+                out=wg[u][:, lo:hi, :].rearrange("p (c i) t -> p c t i", i=4),
+                in_=raw[u][:, :, lo:hi].rearrange("p t (c i) -> p c t i", i=4),
+            )
+
+        def regroup_wide_gpsimd(u):
+            one = stat_pool.tile([P, 1], F32, name="one%d" % u, tag="one")
+            nc.vector.memset(one[:], 1.0)
+            for h in range(2):
+                lo = h * (GPS_COLS // 2)
+                hi = lo + GPS_COLS // 2
+                nc.gpsimd.tensor_scalar(
+                    out=wg[u][:, lo:hi, :],
+                    in0=raw[u][:, :, lo:hi].rearrange("p t w -> p w t"),
+                    scalar1=one[:],
+                    scalar2=0.0,
+                    op0=ALU.mult,
+                    op1=ALU.add,
+                )
 
         def quantise(u):
             s, c = divmod(u, PASSES)
@@ -348,18 +382,20 @@ def tile_quantumsuperposition_kernel(
                     op1=ALU.mult,
                 )
 
-        def inverse_std(n):
-            tot = stat_pool.tile([P, 1], F32, name="tot%d" % n, tag="tot")
-            rstd[n] = stat_pool.tile([P, 1], F32, name="rstd%d" % n, tag="rstd")
-            nc.gpsimd.tensor_scalar(
-                out=tot[:],
+        def variance(n):
+            tot[n] = stat_pool.tile([P, 1], F32, name="tot%d" % n, tag="tot")
+            nc.vector.tensor_scalar(
+                out=tot[n][:],
                 in0=varsum[n][:, 0:1],
                 scalar1=varsum[n][:, 1:2],
                 scalar2=Q * LN_EPS,
                 op0=ALU.add,
                 op1=ALU.add,
             )
-            nc.gpsimd.tensor_tensor(out=rstd[n][:], in0=tot[:], in1=neghalf[:], op=ALU.pow)
+
+        def inverse_std(n):
+            rstd[n] = stat_pool.tile([P, 1], F32, name="rstd%d" % n, tag="rstd")
+            nc.scalar.activation(out=rstd[n][:], in_=tot[n][:], func=ACT.Abs_reciprocal_sqrt)
 
         def finish(n):
             s, bt = divmod(n, BT)
@@ -368,12 +404,14 @@ def tile_quantumsuperposition_kernel(
             )
             nc.sync.dma_start(out=out[bt * P : (bt + 1) * P, s, :], in_=ysb[n][:])
 
-        for n in range(-LEAD_RG, GROUPS + FIN_LAG):
+        for n in range(-LEAD_RG, GROUPS + 1):
             m = n + LEAD_MX
             r = n + LEAD_RG
             nxt = n + 1
             if 0 <= n < GROUPS:
                 squares(n)
+            if 0 <= n - 1 < GROUPS:
+                inverse_std(n - 1)
             if 0 <= m - 1 < GROUPS:
                 mix_out((m - 1) // 4, 2 * ((m - 1) % 4) + 1)
 
@@ -400,22 +438,36 @@ def tile_quantumsuperposition_kernel(
                 nc.vector.tensor_scalar(
                     out=gamma_bc[:], in0=gamma_ps[:], scalar1=math.sqrt(Q), scalar2=None, op0=ALU.mult
                 )
-            if r < 2 * UNITS:
+            narrow = r < 2 * FIRST_WIDE
+            wide = 2 * FIRST_WIDE <= r < 2 * UNITS
+            if narrow:
                 regroup(r // 2, r % 2)
+            if wide and r % 2 == 0:
+                regroup_wide_vector(r // 2)
+            if wide:
+                regroup_wide_scalar(r // 2, r % 2)
             if r == 3:
                 x_quantise(x_grouped)
             if r == 4:
                 parameters_end()
+            if r == 5:
+                nc.scalar.activation(out=warm[:], in_=warm[:], func=ACT.Abs_reciprocal_sqrt)
             if r >= 2 and r % 2 == 0 and r <= 2 * UNITS:
                 quantise(r // 2 - 1)
-            if r < 2 * UNITS:
+            if narrow:
                 regroup_gpsimd(r // 2, r % 2)
-                if r % 2 == 1 and r // 2 + RAW_BUFS < UNITS:
-                    load_unit(r // 2 + RAW_BUFS)
+            if wide and r % 2 == 0:
+                regroup_wide_gpsimd(r // 2)
+            if r < 2 * UNITS and r % 2 == 1 and r // 2 + RAW_BUFS < UNITS:
+                load_unit(r // 2 + RAW_BUFS)
             if 0 <= m < GROUPS:
                 mix_out(m // 4, 2 * (m % 4))
+            if wide and r % 2 == 1 and n >= 2:
+                finish(n - 2)
             if 0 <= n < GROUPS:
                 centre(n)
-                inverse_std(n)
-            if 0 <= n - FIN_LAG < GROUPS:
-                finish(n - FIN_LAG)
+                variance(n)
+            if wide and r % 2 == 1:
+                finish(n - 1)
+            if not wide and 0 <= n - 1 < GROUPS:
+                finish(n - 1)

@@ -27,8 +27,9 @@ UNITS = S * PASSES
 LEAD_MX = 6
 LEAD_RG = 12
 FIRST_WIDE = 6
-GPS_COLS = 592
-SCA_COLS = 240
+FIRST_TAIL = 2 * UNITS - LEAD_RG
+GPS_COLS = 704
+SCA_COLS = 208
 RAW_BUFS = 6
 
 TWO_PI_HI = 6.28125
@@ -71,16 +72,21 @@ def tile_quantumsuperposition_kernel(
         nc.scalar.activation(out=warm[:], in_=neghalf[:], func=ACT.Exp)
 
         raw = {}
+        raw_half = {}
 
         def load_unit(u):
             s, c = divmod(u, PASSES)
             t = raw_pool.tile([P, 4, Q], BF16, name="raw%d" % u, tag="raw")
             rows = W[s, c * 512 : (c + 1) * 512, :].rearrange("(p j) q -> p j q", j=4)
             if u == 0:
+                halves = t[:].rearrange("p t q -> p (t q)").rearrange("p (h t q) -> p h t q", h=2, t=4)
                 for h in range(2):
-                    nc.sync.dma_start(out=t[:, :, h * 512 : (h + 1) * 512], in_=rows[:, :, h * 512 : (h + 1) * 512])
+                    nc.sync.dma_start(out=halves[:, h, :, :], in_=rows[:, :, h * 512 : (h + 1) * 512])
+                    raw_half[u, h] = halves[:, h, :, :]
             else:
                 nc.sync.dma_start(out=t[:], in_=rows)
+                for h in range(2):
+                    raw_half[u, h] = t[:, :, h * 512 : (h + 1) * 512]
             raw[u] = t
 
         load_unit(0)
@@ -147,6 +153,7 @@ def tile_quantumsuperposition_kernel(
 
         gamma_bc = const.tile([P, Q], BF16, name="gamma_bc")
         beta_ps = ps_beta.tile([P, Q], BF16, name="beta_ps")
+        beta_sb = const.tile([P, Q], BF16, name="beta_sb")
 
         def gamma_beta_spread():
             gamma_ps = ps_sup.tile([P, Q], BF16, name="gamma_ps", tag="sup")
@@ -221,43 +228,21 @@ def tile_quantumsuperposition_kernel(
         tot = {}
         rstd = {}
 
-        def shares(piece):
-            if piece < 5:
-                return 0, 264
-            if piece < 11:
-                return 0, 96
-            return 224, 136
+        def scalar_share(piece):
+            return 264 if piece < 5 else 96
 
         def regroup(u, h):
             if h == 0:
                 wg[u] = wg_pool.tile([P, Q, 4], BF16, name="wg%d" % u, tag="wg", align_bytes=64)
-            g_cols, s_cols = shares(2 * u + h)
-            lo = h * 512 + g_cols
-            mid = lo + s_cols
-            hi = (h + 1) * 512
+            mid = scalar_share(2 * u + h)
+            base = h * 512
             nc.scalar.copy(
-                out=wg[u][:, lo:mid, :].rearrange("p (c i) t -> p c t i", i=4),
-                in_=raw[u][:, :, lo:mid].rearrange("p t (c i) -> p c t i", i=4),
+                out=wg[u][:, base : base + mid, :].rearrange("p (c i) t -> p c t i", i=4),
+                in_=raw_half[u, h][:, :, 0:mid].rearrange("p t (c i) -> p c t i", i=4),
             )
             nc.vector.tensor_copy(
-                out=wg[u][:, mid:hi, :].rearrange("p (c i) t -> p c t i", i=4),
-                in_=raw[u][:, :, mid:hi].rearrange("p t (c i) -> p c t i", i=4),
-            )
-
-        def regroup_gpsimd(u, h):
-            g_cols, s_cols = shares(2 * u + h)
-            if g_cols == 0:
-                return
-            one = stat_pool.tile([P, 1], F32, name="one%d_%d" % (u, h), tag="one")
-            nc.vector.memset(one[:], 1.0)
-            lo = h * 512
-            nc.gpsimd.tensor_scalar(
-                out=wg[u][:, lo : lo + g_cols, :],
-                in0=raw[u][:, :, lo : lo + g_cols].rearrange("p t w -> p w t"),
-                scalar1=one[:],
-                scalar2=0.0,
-                op0=ALU.mult,
-                op1=ALU.add,
+                out=wg[u][:, base + mid : base + 512, :].rearrange("p (c i) t -> p c t i", i=4),
+                in_=raw_half[u, h][:, :, mid:512].rearrange("p t (c i) -> p c t i", i=4),
             )
 
         def regroup_wide_vector(u):
@@ -397,11 +382,23 @@ def tile_quantumsuperposition_kernel(
             rstd[n] = stat_pool.tile([P, 1], F32, name="rstd%d" % n, tag="rstd")
             nc.scalar.activation(out=rstd[n][:], in_=tot[n][:], func=ACT.Abs_reciprocal_sqrt)
 
+        def on_gpsimd(n):
+            return FIRST_TAIL <= n < GROUPS and (n - FIRST_TAIL) % 3 == 0
+
         def finish(n):
-            s, bt = divmod(n, BT)
+            if on_gpsimd(n):
+                nc.gpsimd.tensor_scalar(
+                    out=ysb[n][:], in0=ysb[n][:], scalar1=rstd[n][:], scalar2=0.0, op0=ALU.mult, op1=ALU.add
+                )
+                nc.gpsimd.tensor_tensor(out=ysb[n][:], in0=ysb[n][:], in1=beta_sb[:], op=ALU.add)
+                return
             nc.vector.scalar_tensor_tensor(
                 out=ysb[n][:], in0=ysb[n][:], scalar=rstd[n][:], in1=beta_ps[:], op0=ALU.mult, op1=ALU.add
             )
+            store(n)
+
+        def store(n):
+            s, bt = divmod(n, BT)
             nc.sync.dma_start(out=out[bt * P : (bt + 1) * P, s, :], in_=ysb[n][:])
 
         for n in range(-LEAD_RG, GROUPS + 1):
@@ -410,8 +407,6 @@ def tile_quantumsuperposition_kernel(
             nxt = n + 1
             if 0 <= n < GROUPS:
                 squares(n)
-            if 0 <= n - 1 < GROUPS:
-                inverse_std(n - 1)
             if 0 <= m - 1 < GROUPS:
                 mix_out((m - 1) // 4, 2 * ((m - 1) % 4) + 1)
 
@@ -440,6 +435,9 @@ def tile_quantumsuperposition_kernel(
                 )
             narrow = r < 2 * FIRST_WIDE
             wide = 2 * FIRST_WIDE <= r < 2 * UNITS
+            quantise_now = r >= 2 and r % 2 == 0 and r <= 2 * UNITS
+            if narrow and quantise_now:
+                quantise(r // 2 - 1)
             if narrow:
                 regroup(r // 2, r % 2)
             if wide and r % 2 == 0:
@@ -451,15 +449,16 @@ def tile_quantumsuperposition_kernel(
             if r == 4:
                 parameters_end()
             if r == 5:
+                nc.scalar.copy(out=beta_sb[:], in_=beta_ps[:])
                 nc.scalar.activation(out=warm[:], in_=warm[:], func=ACT.Abs_reciprocal_sqrt)
-            if r >= 2 and r % 2 == 0 and r <= 2 * UNITS:
+            if quantise_now and not narrow:
                 quantise(r // 2 - 1)
-            if narrow:
-                regroup_gpsimd(r // 2, r % 2)
             if wide and r % 2 == 0:
                 regroup_wide_gpsimd(r // 2)
             if r < 2 * UNITS and r % 2 == 1 and r // 2 + RAW_BUFS < UNITS:
                 load_unit(r // 2 + RAW_BUFS)
+            if 0 <= n - 1 < GROUPS:
+                inverse_std(n - 1)
             if 0 <= m < GROUPS:
                 mix_out(m // 4, 2 * (m % 4))
             if wide and r % 2 == 1 and n >= 2:
@@ -469,5 +468,7 @@ def tile_quantumsuperposition_kernel(
                 variance(n)
             if wide and r % 2 == 1:
                 finish(n - 1)
+            if on_gpsimd(n - 3):
+                store(n - 3)
             if not wide and 0 <= n - 1 < GROUPS:
                 finish(n - 1)

@@ -28,8 +28,8 @@ LEAD_MX = 6
 LEAD_RG = 12
 FIRST_WIDE = 6
 FIRST_TAIL = 2 * UNITS - LEAD_RG
-GPS_COLS = 704
-SCA_COLS = 208
+GPS_COLS = 656
+SCA_COLS = 216
 RAW_BUFS = 6
 
 TWO_PI_HI = 6.28125
@@ -229,7 +229,7 @@ def tile_quantumsuperposition_kernel(
         rstd = {}
 
         def scalar_share(piece):
-            return 264 if piece < 5 else 96
+            return 224 if piece < 5 else 96
 
         def regroup(u, h):
             if h == 0:
@@ -383,7 +383,7 @@ def tile_quantumsuperposition_kernel(
             nc.scalar.activation(out=rstd[n][:], in_=tot[n][:], func=ACT.Abs_reciprocal_sqrt)
 
         def on_gpsimd(n):
-            return FIRST_TAIL <= n < GROUPS and (n - FIRST_TAIL) % 3 == 0
+            return n in (GROUPS - 6, GROUPS - 4)
 
         def finish(n):
             if on_gpsimd(n):

@@ -28,7 +28,7 @@ LEAD_MX = 6
 LEAD_RG = 12
 FIRST_WIDE = 6
 FIRST_TAIL = 2 * UNITS - LEAD_RG
-GPS_COLS = 656
+GPS_COLS = 688
 SCA_COLS = 216
 RAW_BUFS = 6
 
@@ -229,7 +229,7 @@ def tile_quantumsuperposition_kernel(
         rstd = {}
 
         def scalar_share(piece):
-            return 224 if piece < 5 else 96
+            return 240 if piece < 5 else 96
 
         def regroup(u, h):
             if h == 0:
@@ -264,17 +264,14 @@ def tile_quantumsuperposition_kernel(
         def regroup_wide_gpsimd(u):
             one = stat_pool.tile([P, 1], F32, name="one%d" % u, tag="one")
             nc.vector.memset(one[:], 1.0)
-            for h in range(2):
-                lo = h * (GPS_COLS // 2)
-                hi = lo + GPS_COLS // 2
-                nc.gpsimd.tensor_scalar(
-                    out=wg[u][:, lo:hi, :],
-                    in0=raw[u][:, :, lo:hi].rearrange("p t w -> p w t"),
-                    scalar1=one[:],
-                    scalar2=0.0,
-                    op0=ALU.mult,
-                    op1=ALU.add,
-                )
+            nc.gpsimd.tensor_scalar(
+                out=wg[u][:, 0:GPS_COLS, :],
+                in0=raw[u][:, :, 0:GPS_COLS].rearrange("p t w -> p w t"),
+                scalar1=one[:],
+                scalar2=0.0,
+                op0=ALU.mult,
+                op1=ALU.add,
+            )
 
         def quantise(u):
             s, c = divmod(u, PASSES)
@@ -391,6 +388,20 @@ def tile_quantumsuperposition_kernel(
                     out=ysb[n][:], in0=ysb[n][:], scalar1=rstd[n][:], scalar2=0.0, op0=ALU.mult, op1=ALU.add
                 )
                 nc.gpsimd.tensor_tensor(out=ysb[n][:], in0=ysb[n][:], in1=beta_sb[:], op=ALU.add)
+                return
+            if n == GROUPS - 1:
+                s, bt = divmod(n, BT)
+                for h in range(2):
+                    half = slice(h * 512, (h + 1) * 512)
+                    nc.vector.scalar_tensor_tensor(
+                        out=ysb[n][:, half],
+                        in0=ysb[n][:, half],
+                        scalar=rstd[n][:],
+                        in1=beta_ps[:, half],
+                        op0=ALU.mult,
+                        op1=ALU.add,
+                    )
+                    nc.sync.dma_start(out=out[bt * P : (bt + 1) * P, s, half], in_=ysb[n][:, half])
                 return
             nc.vector.scalar_tensor_tensor(
                 out=ysb[n][:], in0=ysb[n][:], scalar=rstd[n][:], in1=beta_ps[:], op0=ALU.mult, op1=ALU.add

@@ -91,9 +91,10 @@ def tile_quantumsuperposition_kernel(
 
         load_unit(0)
         x_sb = const.tile([P, BT * I], BF16, name="x_sb")
-        nc.sync.dma_start(
-            out=x_sb[:].rearrange("p (t k) -> p t k", t=BT), in_=language_features.rearrange("(t p) k -> p t k", p=P)
-        )
+        x_rows = language_features.rearrange("(t p) k -> p t k", p=P)
+        x_tiles = x_sb[:].rearrange("p (t k) -> p t k", t=BT)
+        for h in range(2):
+            nc.sync.dma_start(out=x_tiles[:, 2 * h : 2 * h + 2, :], in_=x_rows[:, 2 * h : 2 * h + 2, :])
         nc.sync.dma_start(out=gb_row[0:1, 0:Q], in_=ln_gamma.rearrange("(o q) -> o q", o=1))
         nc.sync.dma_start(out=gb_row[0:1, Q : 2 * Q], in_=ln_beta.rearrange("(o q) -> o q", o=1))
         for u in range(1, RAW_BUFS):
@@ -173,31 +174,26 @@ def tile_quantumsuperposition_kernel(
         aex = small.tile([P, 64], F32, name="aex")
         cosv = small.tile([P, 64], F32, name="cosv")
 
-        def x_prepare():
-            xw = x_sb[:].bitcast(F32).rearrange("p (t g w u) -> p t g u w", t=BT, g=PASSES, u=2)
-            xg = []
-            for g in range(PASSES):
-                xg_g = const.tile([P, 4 * B], BF16, name="xg%d" % g, align_bytes=64)
-                xg.append(xg_g)
-                xg_words = xg_g[:].bitcast(F32).rearrange("p (r u) -> p r u", u=2)
-                for h in range(2):
-                    xt = ps_sup.tile([P, 2, 256], F32, name="xt%d%d" % (g, h), tag="sup")
-                    for bl in range(2):
-                        for u in range(2):
-                            nc.tensor.transpose(
-                                out=xt[:, u, bl * P : (bl + 1) * P], in_=xw[:, 2 * h + bl, g, u, :], identity=ident[:]
-                            )
-                    dst = xg_words[:, h * 256 : (h + 1) * 256, :]
-                    src = xt[:].rearrange("p u r -> p r u")
-                    if h == 0:
-                        nc.vector.tensor_copy(out=dst, in_=src)
-                    else:
-                        nc.scalar.copy(out=dst, in_=src)
-            return xg
+        xg = [const.tile([P, 4 * B], BF16, name="xg%d" % g, align_bytes=64) for g in range(PASSES)]
 
-        def x_quantise(xg):
+        def x_turn(h):
+            xw = x_sb[:].bitcast(F32).rearrange("p (t g w u) -> p t g u w", t=BT, g=PASSES, u=2)
             for g in range(PASSES):
-                nc.vector.quantize_mx(out=xc[:, g, :].bitcast(FP8X4), scales=xs[:, g, :], in_=xg[g][:])
+                xt = ps_sup.tile([P, 2, 256], F32, name="xt%d%d" % (g, h), tag="sup")
+                for bl in range(2):
+                    for u in range(2):
+                        nc.tensor.transpose(
+                            out=xt[:, u, bl * P : (bl + 1) * P], in_=xw[:, 2 * h + bl, g, u, :], identity=ident[:]
+                        )
+                dst = xg[g][:].bitcast(F32).rearrange("p (r u) -> p r u", u=2)[:, h * 256 : (h + 1) * 256, :]
+                src = xt[:].rearrange("p u r -> p r u")
+                if g == 0:
+                    nc.vector.tensor_copy(out=dst, in_=src)
+                else:
+                    nc.scalar.copy(out=dst, in_=src)
+
+        def x_quantise(g):
+            nc.vector.quantize_mx(out=xc[:, g, :].bitcast(FP8X4), scales=xs[:, g, :], in_=xg[g][:])
 
         def parameters_middle():
             nc.scalar.activation(out=aex[:], in_=ash[:], func=ACT.Exp)
@@ -205,14 +201,23 @@ def tile_quantumsuperposition_kernel(
         mix_t = const.tile([P, 64], F32, name="mix_t")
         bmix_t = const.tile([P, 64], F32, name="bmix_t")
 
-        def parameters_end():
-            asum = small.tile([P, QT], F32, name="asum")
+        asum = small.tile([P, QT], F32, name="asum")
+        arec = small.tile([P, QT], F32, name="arec")
+        ampl = small.tile([P, 64], F32, name="ampl")
+
+        def softmax_sum():
             nc.vector.tensor_reduce(out=asum[:], in_=ts(aex[:]), axis=AX.X, op=ALU.add)
-            arec = small.tile([P, QT], F32, name="arec")
+
+        def softmax_reciprocal():
             nc.vector.reciprocal(out=arec[:], in_=asum[:])
-            ampl = small.tile([P, 64], F32, name="ampl")
+
+        def softmax_scale():
             nc.vector.tensor_tensor(out=st(ampl[:]), in0=st(aex[:]), in1=over_s(arec[:]), op=ALU.mult)
+
+        def mix_factor():
             nc.vector.tensor_tensor(out=mix_t[:], in0=ampl[:], in1=cosv[:], op=ALU.mult)
+
+        def mix_bias():
             nc.vector.tensor_tensor(out=bmix_t[:], in0=bias_t, in1=mix_t[:], op=ALU.mult)
 
         wg = {}
@@ -438,7 +443,9 @@ def tile_quantumsuperposition_kernel(
             if r == 2:
                 parameters_begin()
                 parameters_middle()
-                x_grouped = x_prepare()
+                x_turn(0)
+                quantise(0)
+                x_turn(1)
                 gamma_ps = gamma_beta_spread()
             if r == 6:
                 nc.vector.tensor_scalar(
@@ -447,8 +454,10 @@ def tile_quantumsuperposition_kernel(
             narrow = r < 2 * FIRST_WIDE
             wide = 2 * FIRST_WIDE <= r < 2 * UNITS
             quantise_now = r >= 2 and r % 2 == 0 and r <= 2 * UNITS
-            if narrow and quantise_now:
+            if narrow and quantise_now and r > 2:
                 quantise(r // 2 - 1)
+            if r == 4:
+                mix_factor()
             if narrow:
                 regroup(r // 2, r % 2)
             if wide and r % 2 == 0:
@@ -456,11 +465,14 @@ def tile_quantumsuperposition_kernel(
             if wide:
                 regroup_wide_scalar(r // 2, r % 2)
             if r == 3:
-                x_quantise(x_grouped)
+                softmax_sum()
+                x_quantise(0)
+                softmax_reciprocal()
+                x_quantise(1)
+                softmax_scale()
             if r == 4:
-                parameters_end()
+                mix_bias()
             if r == 5:
-                nc.scalar.copy(out=beta_sb[:], in_=beta_ps[:])
                 nc.scalar.activation(out=warm[:], in_=warm[:], func=ACT.Abs_reciprocal_sqrt)
             if quantise_now and not narrow:
                 quantise(r // 2 - 1)
@@ -472,6 +484,8 @@ def tile_quantumsuperposition_kernel(
                 inverse_std(n - 1)
             if 0 <= m < GROUPS:
                 mix_out(m // 4, 2 * (m % 4))
+            if m == GROUPS:
+                nc.scalar.copy(out=beta_sb[:], in_=beta_ps[:])
             if wide and r % 2 == 1 and n >= 2:
                 finish(n - 2)
             if 0 <= n < GROUPS:

@@ -480,12 +480,12 @@ def tile_quantumsuperposition_kernel(
                 regroup_wide_gpsimd(r // 2)
             if r < 2 * UNITS and r % 2 == 1 and r // 2 + RAW_BUFS < UNITS:
                 load_unit(r // 2 + RAW_BUFS)
+            if n == FIRST_TAIL - 8:
+                nc.sync.dma_start(out=beta_sb[:], in_=ln_beta.partition_broadcast(P))
             if 0 <= n - 1 < GROUPS:
                 inverse_std(n - 1)
             if 0 <= m < GROUPS:
                 mix_out(m // 4, 2 * (m % 4))
-            if m == GROUPS:
-                nc.scalar.copy(out=beta_sb[:], in_=beta_ps[:])
             if wide and r % 2 == 1 and n >= 2:
                 finish(n - 2)
             if 0 <= n < GROUPS:

import math
from contextlib import ExitStack

import concourse.mybir as mybir
from concourse.masks import make_identity

FP8X4 = mybir.dt.float8_e4m3fn_x4
BF16 = mybir.dt.bfloat16
F32 = mybir.dt.float32
I32 = mybir.dt.int32
U32 = mybir.dt.uint32
U8 = mybir.dt.uint8
ACT = mybir.ActivationFunctionType
ALU = mybir.AluOpType
AX = mybir.AxisListType

P = 128
B, S, I, Q = 512, 8, 1024, 1024
LN_EPS = 1e-5
FLOPS = 2 * B * S * I * Q

PASSES = I // 512
QT = Q // P
BT = B // P
GROUPS = S * BT
UNITS = S * PASSES
LEAD_MX = 6
LEAD_RG = 12
FIRST_WIDE = 6
FIRST_TAIL = 2 * UNITS - LEAD_RG
GPS_COLS = 688
SCA_COLS = 216
RAW_BUFS = 6

TWO_PI_HI = 6.28125
TWO_PI_LO = 2.0 * math.pi - 6.28125
PI_BELOW = 3.1415925


def tile_quantumsuperposition_kernel(
    tc, language_features, W, b, amplitude_weights, phase_weights, ln_gamma, ln_beta, out
):
    nc = tc.nc
    with ExitStack() as ctx:
        ctx.enter_context(tc.manual_schedule())
        const = ctx.enter_context(tc.tile_pool(name="const", bufs=1))
        small = ctx.enter_context(tc.tile_pool(name="small", bufs=1))
        raw_pool = ctx.enter_context(tc.tile_pool(name="raw", bufs=RAW_BUFS))
        wg_pool = ctx.enter_context(tc.tile_pool(name="wg", bufs=3))
        code_pool = ctx.enter_context(tc.tile_pool(name="codes", bufs=3))
        supt_pool = ctx.enter_context(tc.tile_pool(name="supt", bufs=3))
        y_pool = ctx.enter_context(tc.tile_pool(name="y", bufs=7))
        stat_pool = ctx.enter_context(tc.tile_pool(name="stat", bufs=4))
        ps_acc = ctx.enter_context(tc.psum_pool(name="ps_acc", bufs=2))
        ps_sup = ctx.enter_context(tc.psum_pool(name="ps_sup", bufs=4))
        ps_sum = ctx.enter_context(tc.psum_pool(name="ps_sum", bufs=1))
        ps_beta = ctx.enter_context(tc.psum_pool(name="ps_beta", bufs=1))

        par_a = small.tile([P, P], BF16, name="par_a")
        par_b = small.tile([P, P], BF16, name="par_b")
        gb_row = small.tile([P, 2 * Q], BF16, name="gb_row")
        ones_bf = small.tile([P, P], BF16, name="ones_bf")
        neghalf = const.tile([P, 1], F32, name="neghalf")
        nc.vector.memset(neghalf[:], -0.5)
        nc.vector.memset(par_b[64:128, :], 0.0)
        nc.vector.memset(ones_bf[:], 1.0)
        nc.vector.memset(gb_row[:], 0.0)
        nc.scalar.dma_start(out=par_a[0:64, :], in_=amplitude_weights.rearrange("s (t q) -> (s t) q", q=P))
        nc.scalar.dma_start(out=par_a[64:128, :], in_=phase_weights.rearrange("s (t q) -> (s t) q", q=P))
        nc.sync.dma_start(out=par_b[0:64, :], in_=b.rearrange("s (t q) -> (s t) q", q=P))
        warm = small.tile([P, 1], F32, name="warm")
        nc.scalar.activation(out=warm[:], in_=neghalf[:], func=ACT.Exp)

        raw = {}
        raw_half = {}

        def load_unit(u):
            s, c = divmod(u, PASSES)
            t = raw_pool.tile([P, 4, Q], BF16, name="raw%d" % u, tag="raw")
            rows = W[s, c * 512 : (c + 1) * 512, :].rearrange("(p j) q -> p j q", j=4)
            if u == 0:
                halves = t[:].rearrange("p t q -> p (t q)").rearrange("p (h t q) -> p h t q", h=2, t=4)
                for h in range(2):
                    nc.sync.dma_start(out=halves[:, h, :, :], in_=rows[:, :, h * 512 : (h + 1) * 512])
                    raw_half[u, h] = halves[:, h, :, :]
            else:
                nc.sync.dma_start(out=t[:], in_=rows)
                for h in range(2):
                    raw_half[u, h] = t[:, :, h * 512 : (h + 1) * 512]
            raw[u] = t

        load_unit(0)
        x_sb = const.tile([P, BT * I], BF16, name="x_sb")
        x_rows = language_features.rearrange("(t p) k -> p t k", p=P)
        x_tiles = x_sb[:].rearrange("p (t k) -> p t k", t=BT)
        for h in range(2):
            nc.sync.dma_start(out=x_tiles[:, 2 * h : 2 * h + 2, :], in_=x_rows[:, 2 * h : 2 * h + 2, :])
        nc.sync.dma_start(out=gb_row[0:1, 0:Q], in_=ln_gamma.rearrange("(o q) -> o q", o=1))
        nc.sync.dma_start(out=gb_row[0:1, Q : 2 * Q], in_=ln_beta.rearrange("(o q) -> o q", o=1))
        for u in range(1, RAW_BUFS):
            load_unit(u)

        ident = const.tile([P, P], F32, name="ident")
        make_identity(nc, ident[:])
        ident_bf = const.tile([P, P], BF16, name="ident_bf")
        nc.vector.tensor_copy(out=ident_bf[:], in_=ident[:])

        prm = small.tile([P, 192], F32, name="prm")
        amp_t = prm[:, 0:64]
        pha_t = prm[:, 64:128]
        bias_t = prm[:, 128:192]
        ash = small.tile([P, 64], F32, name="ash")
        ang_clip = small.tile([P, 64], F32, name="ang_clip")

        def st(ap):
            return ap.rearrange("p (s t) -> p s t", s=S)

        def ts(ap):
            return ap.rearrange("p (s t) -> p t s", s=S)

        def over_s(ap):
            return ap.unsqueeze(1).to_broadcast([P, S, QT])

        def parameters_begin():
            par_ps = ps_acc.tile([P, 2 * P], BF16, name="par_ps", tag="acc")
            nc.tensor.transpose(out=par_ps[:, 0:P], in_=par_a[:], identity=ident_bf[:])
            nc.tensor.transpose(out=par_ps[:, P : 2 * P], in_=par_b[:], identity=ident_bf[:])
            nc.vector.tensor_copy(out=prm[:], in_=par_ps[:, 0:192])

            turns = small.tile([P, 64], F32, name="turns")
            nc.vector.tensor_scalar(
                out=turns[:], in0=pha_t, scalar1=1.0 / (2.0 * math.pi), scalar2=0.25, op0=ALU.mult, op1=ALU.add
            )
            amax = small.tile([P, QT], F32, name="amax")
            nc.vector.tensor_reduce(out=amax[:], in_=ts(amp_t), axis=AX.X, op=ALU.max)
            turns_i = small.tile([P, 64], I32, name="turns_i")
            nc.vector.tensor_copy(out=turns_i[:], in_=turns[:])
            nc.vector.tensor_tensor(out=st(ash[:]), in0=st(amp_t), in1=over_s(amax[:]), op=ALU.subtract)
            turns_f = small.tile([P, 64], F32, name="turns_f")
            nc.vector.tensor_copy(out=turns_f[:], in_=turns_i[:])
            ang0 = small.tile([P, 64], F32, name="ang0")
            nc.vector.tensor_scalar(out=ang0[:], in0=pha_t, scalar1=0.5 * math.pi, scalar2=None, op0=ALU.add)
            ang1 = small.tile([P, 64], F32, name="ang1")
            nc.vector.scalar_tensor_tensor(
                out=ang1[:], in0=turns_f[:], scalar=-TWO_PI_HI, in1=ang0[:], op0=ALU.mult, op1=ALU.add
            )
            ang2 = small.tile([P, 64], F32, name="ang2")
            nc.vector.scalar_tensor_tensor(
                out=ang2[:], in0=turns_f[:], scalar=-TWO_PI_LO, in1=ang1[:], op0=ALU.mult, op1=ALU.add
            )
            nc.vector.tensor_scalar(
                out=ang_clip[:], in0=ang2[:], scalar1=-PI_BELOW, scalar2=PI_BELOW, op0=ALU.max, op1=ALU.min
            )

        gamma_bc = const.tile([P, Q], BF16, name="gamma_bc")
        beta_ps = ps_beta.tile([P, Q], BF16, name="beta_ps")
        beta_sb = const.tile([P, Q], BF16, name="beta_sb")

        def gamma_beta_spread():
            gamma_ps = ps_sup.tile([P, Q], BF16, name="gamma_ps", tag="sup")
            for k, dst_ps in enumerate((gamma_ps, beta_ps)):
                for h in range(2):
                    nc.tensor.matmul(
                        out=dst_ps[:, h * 512 : (h + 1) * 512],
                        lhsT=ones_bf[:],
                        rhs=gb_row[:, k * Q + h * 512 : k * Q + (h + 1) * 512],
                        start=True,
                        stop=True,
                    )
            return gamma_ps

        xc = const.tile([P, PASSES, B], U32, name="xc", align_bytes=64)
        xs = const.tile([P, PASSES, B], U8, name="xs", align_bytes=64)
        aex = small.tile([P, 64], F32, name="aex")
        cosv = small.tile([P, 64], F32, name="cosv")

        xg = [const.tile([P, 4 * B], BF16, name="xg%d" % g, align_bytes=64) for g in range(PASSES)]

        def x_turn(h):
            xw = x_sb[:].bitcast(F32).rearrange("p (t g w u) -> p t g u w", t=BT, g=PASSES, u=2)
            for g in range(PASSES):
                xt = ps_sup.tile([P, 2, 256], F32, name="xt%d%d" % (g, h), tag="sup")
                for bl in range(2):
                    for u in range(2):
                        nc.tensor.transpose(
                            out=xt[:, u, bl * P : (bl + 1) * P], in_=xw[:, 2 * h + bl, g, u, :], identity=ident[:]
                        )
                dst = xg[g][:].bitcast(F32).rearrange("p (r u) -> p r u", u=2)[:, h * 256 : (h + 1) * 256, :]
                src = xt[:].rearrange("p u r -> p r u")
                if g == 0:
                    nc.vector.tensor_copy(out=dst, in_=src)
                else:
                    nc.scalar.copy(out=dst, in_=src)

        def x_quantise(g):
            nc.vector.quantize_mx(out=xc[:, g, :].bitcast(FP8X4), scales=xs[:, g, :], in_=xg[g][:])

        def parameters_middle():
            nc.scalar.activation(out=aex[:], in_=ash[:], func=ACT.Exp)
            nc.scalar.activation(out=cosv[:], in_=ang_clip[:], func=ACT.Sin)
        mix_t = const.tile([P, 64], F32, name="mix_t")
        bmix_t = const.tile([P, 64], F32, name="bmix_t")

        asum = small.tile([P, QT], F32, name="asum")
        arec = small.tile([P, QT], F32, name="arec")
        ampl = small.tile([P, 64], F32, name="ampl")

        def softmax_sum():
            nc.vector.tensor_reduce(out=asum[:], in_=ts(aex[:]), axis=AX.X, op=ALU.add)

        def softmax_reciprocal():
            nc.vector.reciprocal(out=arec[:], in_=asum[:])

        def softmax_scale():
            nc.vector.tensor_tensor(out=st(ampl[:]), in0=st(aex[:]), in1=over_s(arec[:]), op=ALU.mult)

        def mix_factor():
            nc.vector.tensor_tensor(out=mix_t[:], in0=ampl[:], in1=cosv[:], op=ALU.mult)

        def mix_bias():
            nc.vector.tensor_tensor(out=bmix_t[:], in0=bias_t, in1=mix_t[:], op=ALU.mult)

        wg = {}
        wc = {}
        ws = {}
        supt = {}
        acc = {}
        sup = {}
        sums = {}
        ysb = {}
        negmean = {}
        varsum = {}
        tot = {}
        rstd = {}

        def scalar_share(piece):
            return 240 if piece < 5 else 96

        def regroup(u, h):
            if h == 0:
                wg[u] = wg_pool.tile([P, Q, 4], BF16, name="wg%d" % u, tag="wg", align_bytes=64)
            mid = scalar_share(2 * u + h)
            base = h * 512
            nc.scalar.copy(
                out=wg[u][:, base : base + mid, :].rearrange("p (c i) t -> p c t i", i=4),
                in_=raw_half[u, h][:, :, 0:mid].rearrange("p t (c i) -> p c t i", i=4),
            )
            nc.vector.tensor_copy(
                out=wg[u][:, base + mid : base + 512, :].rearrange("p (c i) t -> p c t i", i=4),
                in_=raw_half[u, h][:, :, mid:512].rearrange("p t (c i) -> p c t i", i=4),
            )

        def regroup_wide_vector(u):
            wg[u] = wg_pool.tile([P, Q, 4], BF16, name="wg%d" % u, tag="wg", align_bytes=64)
            lo = GPS_COLS + SCA_COLS
            nc.vector.tensor_copy(
                out=wg[u][:, lo:Q, :].rearrange("p (c i) t -> p c t i", i=4),
                in_=raw[u][:, :, lo:Q].rearrange("p t (c i) -> p c t i", i=4),
            )

        def regroup_wide_scalar(u, h):
            lo = GPS_COLS + h * (SCA_COLS // 2)
            hi = lo + SCA_COLS // 2
            nc.scalar.copy(
                out=wg[u][:, lo:hi, :].rearrange("p (c i) t -> p c t i", i=4),
                in_=raw[u][:, :, lo:hi].rearrange("p t (c i) -> p c t i", i=4),
            )

        def regroup_wide_gpsimd(u):
            one = stat_pool.tile([P, 1], F32, name="one%d" % u, tag="one")
            nc.vector.memset(one[:], 1.0)
            nc.gpsimd.tensor_scalar(
                out=wg[u][:, 0:GPS_COLS, :],
                in0=raw[u][:, :, 0:GPS_COLS].rearrange("p t w -> p w t"),
                scalar1=one[:],
                scalar2=0.0,
                op0=ALU.mult,
                op1=ALU.add,
            )

        def quantise(u):
            s, c = divmod(u, PASSES)
            if c == 0:
                wc[s] = code_pool.tile([P, PASSES, Q], U32, name="wc%d" % s, tag="wc", align_bytes=64)
                ws[s] = code_pool.tile([P, PASSES, Q], U8, name="ws%d" % s, tag="ws", align_bytes=64)
            nc.vector.quantize_mx(
                out=wc[s][:, c, :].bitcast(FP8X4),
                scales=ws[s][:, c, :],
                in_=wg[u][:].rearrange("p w j -> p (w j)"),
            )

        def mx_pass(s, qt, c):
            if c == 0:
                acc[s, qt] = ps_acc.tile([P, B], F32, name="acc%d_%d" % (s, qt), tag="acc")
            cols = slice(qt * P, (qt + 1) * P)
            nc.tensor.matmul_mx(
                out=acc[s, qt][:],
                lhsT=wc[s][:, c, cols].bitcast(FP8X4),
                lhsT_scale=ws[s][:, c, cols],
                rhs=xc[:, c, :].bitcast(FP8X4),
                rhs_scale=xs[:, c, :],
                start=(c == 0),
                stop=(c == PASSES - 1),
            )

        def mix_out(s, qt):
            if qt == 0:
                supt[s] = supt_pool.tile([P, QT, B], F32, name="supt%d" % s, tag="supt")
            col = s * QT + qt
            nc.scalar.activation(
                out=supt[s][:, qt, :],
                in_=acc[s, qt][:],
                func=ACT.Identity,
                scale=mix_t[:, col : col + 1],
                bias=bmix_t[:, col : col + 1],
            )

        def turn_one(n, qt):
            s, bt = divmod(n, BT)
            if qt == 0:
                sup[n] = [ps_sup.tile([P, 512], F32, name="sup%d_%d" % (n, h), tag="sup") for h in range(2)]
            nc.tensor.transpose(
                out=sup[n][qt // 4][:, (qt % 4) * P : (qt % 4 + 1) * P],
                in_=supt[s][:, qt, bt * P : (bt + 1) * P],
                identity=ident[:],
            )

        def turn_add(n, qt):
            s, bt = divmod(n, BT)
            if qt == 0:
                sums[n] = ps_sum.tile([P, P], F32, name="sums%d" % n, tag="sums")
            nc.tensor.matmul(
                out=sums[n][:],
                lhsT=supt[s][:, qt, bt * P : (bt + 1) * P],
                rhs=ident[:],
                start=(qt == 0),
                stop=(qt == QT - 1),
                is_transpose=True,
            )

        def mean_of(n):
            junk = stat_pool.tile([P, P], F32, name="junk%d" % n, tag="junk")
            negmean[n] = stat_pool.tile([P, 1], F32, name="negmean%d" % n, tag="negmean")
            nc.scalar.activation(
                out=junk[:], in_=sums[n][:], func=ACT.Copy, scale=-1.0 / Q, accum_out=negmean[n][:]
            )

        def squares(n):
            varsum[n] = stat_pool.tile([P, 2], F32, name="varsum%d" % n, tag="varsum")
            ysb[n] = y_pool.tile([P, Q], F32, name="y%d" % n, tag="y")
            for h in range(2):
                nc.scalar.activation(
                    out=ysb[n][:, h * 512 : (h + 1) * 512],
                    in_=sup[n][h][:],
                    func=ACT.Square,
                    bias=negmean[n][:],
                    accum_out=varsum[n][:, h : h + 1],
                )

        def centre(n):
            for h in range(2):
                half = slice(h * 512, (h + 1) * 512)
                nc.vector.scalar_tensor_tensor(
                    out=ysb[n][:, half],
                    in0=sup[n][h][:],
                    scalar=negmean[n][:],
                    in1=gamma_bc[:, half],
                    op0=ALU.add,
                    op1=ALU.mult,
                )

        def variance(n):
            tot[n] = stat_pool.tile([P, 1], F32, name="tot%d" % n, tag="tot")
            nc.vector.tensor_scalar(
                out=tot[n][:],
                in0=varsum[n][:, 0:1],
                scalar1=varsum[n][:, 1:2],
                scalar2=Q * LN_EPS,
                op0=ALU.add,
                op1=ALU.add,
            )

        def inverse_std(n):
            rstd[n] = stat_pool.tile([P, 1], F32, name="rstd%d" % n, tag="rstd")
            nc.scalar.activation(out=rstd[n][:], in_=tot[n][:], func=ACT.Abs_reciprocal_sqrt)

        def on_gpsimd(n):
            return n in (GROUPS - 6, GROUPS - 4)

        def finish(n):
            if on_gpsimd(n):
                nc.gpsimd.tensor_scalar(
                    out=ysb[n][:], in0=ysb[n][:], scalar1=rstd[n][:], scalar2=0.0, op0=ALU.mult, op1=ALU.add
                )
                nc.gpsimd.tensor_tensor(out=ysb[n][:], in0=ysb[n][:], in1=beta_sb[:], op=ALU.add)
                return
            if n == GROUPS - 1:
                s, bt = divmod(n, BT)
                for h in range(2):
                    half = slice(h * 512, (h + 1) * 512)
                    nc.vector.scalar_tensor_tensor(
                        out=ysb[n][:, half],
                        in0=ysb[n][:, half],
                        scalar=rstd[n][:],
                        in1=beta_ps[:, half],
                        op0=ALU.mult,
                        op1=ALU.add,
                    )
                    nc.sync.dma_start(out=out[bt * P : (bt + 1) * P, s, half], in_=ysb[n][:, half])
                return
            nc.vector.scalar_tensor_tensor(
                out=ysb[n][:], in0=ysb[n][:], scalar=rstd[n][:], in1=beta_ps[:], op0=ALU.mult, op1=ALU.add
            )
            store(n)

        def store(n):
            s, bt = divmod(n, BT)
            nc.sync.dma_start(out=out[bt * P : (bt + 1) * P, s, :], in_=ysb[n][:])

        for n in range(-LEAD_RG, GROUPS + 1):
            m = n + LEAD_MX
            r = n + LEAD_RG
            nxt = n + 1
            if 0 <= n < GROUPS:
                squares(n)
            if 0 <= m - 1 < GROUPS:
                mix_out((m - 1) // 4, 2 * ((m - 1) % 4) + 1)

            if 0 <= nxt < GROUPS:
                for qt in range(QT):
                    turn_add(nxt, qt)
            if 0 <= m < GROUPS:
                for c in range(PASSES):
                    mx_pass(m // 4, 2 * (m % 4), c)
            if 0 <= nxt < GROUPS:
                mean_of(nxt)
                for qt in range(QT):
                    turn_one(nxt, qt)
            if 0 <= m < GROUPS:
                for c in range(PASSES):
                    mx_pass(m // 4, 2 * (m % 4) + 1, c)

            if r == 2:
                parameters_begin()
                parameters_middle()
                x_turn(0)
                quantise(0)
                x_turn(1)
                gamma_ps = gamma_beta_spread()
            if r == 6:
                nc.vector.tensor_scalar(
                    out=gamma_bc[:], in0=gamma_ps[:], scalar1=math.sqrt(Q), scalar2=None, op0=ALU.mult
                )
            narrow = r < 2 * FIRST_WIDE
            wide = 2 * FIRST_WIDE <= r < 2 * UNITS
            quantise_now = r >= 2 and r % 2 == 0 and r <= 2 * UNITS
            if narrow and quantise_now and r > 2:
                quantise(r // 2 - 1)
            if r == 4:
                mix_factor()
            if narrow:
                regroup(r // 2, r % 2)
            if wide and r % 2 == 0:
                regroup_wide_vector(r // 2)
            if wide:
                regroup_wide_scalar(r // 2, r % 2)
            if r == 3:
                softmax_sum()
                x_quantise(0)
                softmax_reciprocal()
                x_quantise(1)
                softmax_scale()
            if r == 4:
                mix_bias()
            if r == 5:
                nc.scalar.activation(out=warm[:], in_=warm[:], func=ACT.Abs_reciprocal_sqrt)
            if quantise_now and not narrow:
                quantise(r // 2 - 1)
            if wide and r % 2 == 0:
                regroup_wide_gpsimd(r // 2)
            if r < 2 * UNITS and r % 2 == 1 and r // 2 + RAW_BUFS < UNITS:
                load_unit(r // 2 + RAW_BUFS)
            if n == FIRST_TAIL - 8:
                nc.sync.dma_start(out=beta_sb[:], in_=ln_beta.partition_broadcast(P))
            if 0 <= n - 1 < GROUPS:
                inverse_std(n - 1)
            if 0 <= m < GROUPS:
                mix_out(m // 4, 2 * (m % 4))
            if wide and r % 2 == 1 and n >= 2:
                finish(n - 2)
            if 0 <= n < GROUPS:
                centre(n)
                variance(n)
            if wide and r % 2 == 1:
                finish(n - 1)
            if on_gpsimd(n - 3):
                store(n - 3)
            if not wide and 0 <= n - 1 < GROUPS:
                finish(n - 1)
